import numpy as np
import ml_dtypes


BF16 = ml_dtypes.bfloat16


def bf(x):
    return np.asarray(x, np.float32).astype(BF16)


def f64(x):
    return np.asarray(x).astype(np.float64)


E2M1 = np.array([0.0, 0.5, 1.0, 1.5, 2.0, 3.0, 4.0, 6.0, -0.0, -0.5, -1.0, -1.5, -2.0, -3.0, -4.0, -6.0])


def pack_weight(w, fmt):
    k, n = w.shape
    w = f64(bf(w)).reshape(k // 32, 32, n)
    amax = np.abs(w).max(1)
    if fmt == "e4m3":
        byte = np.frexp(amax)[1] - 1 + 127 - 7
    else:
        mant, ex = np.frexp(amax / 6.0)
        byte = np.where(mant > 0.5, ex, ex - 1) + 127
    byte = np.clip(np.where(amax > 0, byte, 1), 1, 254)
    scaled = (w * np.exp2(127.0 - byte)[:, None, :]).reshape(k, n).astype(np.float32)
    by_word = np.ascontiguousarray(scaled.reshape(k // 512, 128, 4, n).transpose(0, 1, 3, 2))
    if fmt == "e4m3":
        words = by_word.astype(ml_dtypes.float8_e4m3fn).view(np.uint8)
    else:
        c = by_word.astype(ml_dtypes.float4_e2m1fn).view(np.uint8) & 0xF
        words = c[..., 0::2] | (c[..., 1::2] << 4)
    return np.ascontiguousarray(words), np.ascontiguousarray(byte.astype(np.uint8).reshape(k // 512, 16, n))


def unpack_weight(words, scales, fmt):
    g, p, n, _ = words.shape
    if fmt == "e4m3":
        vals = np.ascontiguousarray(words).view(ml_dtypes.float8_e4m3fn).astype(np.float64)
    else:
        nib = np.empty((g, p, n, 4), np.uint8)
        nib[..., 0::2] = words & 0xF
        nib[..., 1::2] = words >> 4
        vals = E2M1[nib]
    vals = vals * np.repeat(np.exp2(scales.astype(np.float64) - 127.0), 8, axis=1)[..., None]
    return vals.transpose(0, 1, 3, 2).reshape(g * 512, n)

def pack4(w):
    words, scales = pack_weight(w, "e2m1")
    return words.reshape(words.shape[0], 128, -1), scales


def unpack4(words, scales):
    return unpack_weight(words.reshape(words.shape[0], 128, -1, 2), scales, "e2m1")


def kspread(k):
    return np.exp2(np.repeat(np.random.randint(-6, 7, k // 32), 32).astype(np.float64))


B, FS, NFPB, NIB, NAPB, NSPB, LOCAL, DIM, NH, RB, HG = 1, 512, 2, 3, 32, 1, 4, 3072, 12, 2048, 2
HD = DIM // NH
EPS = 1e-6


def setup_inputs():
    s = kspread(DIM)
    ang = np.random.uniform(0.0, 2.0 * np.pi, (RB, HD // 2))
    x = np.random.standard_normal((RB, DIM)) * s
    x_words, x_scales = pack4(np.ascontiguousarray(x.reshape(RB, DIM).T))
    w_words, w_scales = pack4(np.random.standard_normal((DIM, DIM)) / np.sqrt(DIM) / s[:, None])
    b = bf(np.random.standard_normal(DIM) * 0.1)
    g = bf(1.5 + 0.15 * np.random.standard_normal(DIM))
    freqs = bf(np.stack([np.cos(ang), np.sin(ang)], axis=-1).reshape(RB, HD))
    return {'x_words': x_words,
            'x_scales': x_scales,
            'w_words': w_words,
            'w_scales': w_scales,
            'b': b,
            'g': g,
            'freqs': freqs}


def reference(x_words, x_scales, w_words, w_scales, b, g, freqs):
    y = (unpack4(x_words, x_scales).T @ unpack4(w_words, w_scales)) + f64(b)
    y = y * (1.0 / np.sqrt(np.mean(np.square(y), axis=-1, keepdims=True) + EPS)) * f64(g)
    yp = y.reshape(RB, NH, HD // 2, 2)
    yr, yi = yp[..., 0], yp[..., 1]
    f = f64(freqs).reshape(RB, HD // 2, 2)
    c, sn = f[:, None, :, 0], f[:, None, :, 1]
    return np.stack([yr * c - yi * sn, yr * sn + yi * c], axis=-1).reshape(RB, NH, HD)

@@ -1,0 +1,269 @@
+from contextlib import ExitStack
+
+import concourse.mybir as mybir
+from concourse.masks import make_identity
+
+ROWS, DIM, HEAD = 2048, 3072, 256
+FLOPS = 2 * ROWS * DIM * DIM
+EPS = 1e-6
+
+F32 = mybir.dt.float32
+BF16 = mybir.dt.bfloat16
+U8 = mybir.dt.uint8
+I32 = mybir.dt.int32
+FP4X4 = mybir.dt.float4_e2m1fn_x4
+ACT = mybir.ActivationFunctionType
+ALU = mybir.AluOpType
+AX = mybir.AxisListType
+
+P = 128
+PASSES = DIM // 512
+CT = DIM // P
+GROUP = 4
+BANK = 512
+BLOCKS = (512, 512, 512, 256, 128, 128)
+TURN_LAG = 2
+FINISH_LAG = 7
+FINISH_STEP = 512
+
+
+def tile_causalwanselfattention_pa_kernel(tc, x_words, x_scales, w_words, w_scales, b, g, freqs, out):
+    nc = tc.nc
+    out_rows = out.rearrange("r h d -> r (h d)")
+
+    with ExitStack() as ctx:
+        keep = ctx.enter_context(tc.tile_pool(name="keep", bufs=1))
+        work = ctx.enter_context(tc.tile_pool(name="work", bufs=2))
+        psum = ctx.enter_context(tc.psum_pool(name="psum", bufs=4))
+        ctx.enter_context(tc.manual_schedule())
+
+        def load_scales(plane, src, cols):
+            nc.vector.memset(plane[:].bitcast(I32), 0)
+            for quad in range(4):
+                nc.sync.dma_start(
+                    out=plane[32 * quad : 32 * quad + 4, :, :].bitcast(I32),
+                    in_=src[:, 4 * quad : 4 * quad + 4, cols].rearrange("k r n -> r k n").bitcast(I32),
+                )
+
+        def load_codes(codes, src, cols):
+            nc.sync.dma_start(out=codes[:].bitcast(I32), in_=src[:, :, cols].rearrange("k p n -> p k n").bitcast(I32))
+
+        starts = [sum(BLOCKS[:i]) for i in range(len(BLOCKS))]
+        staged = {}
+
+        def stage_scales(blk):
+            n = BLOCKS[blk]
+            xs = work.tile([P, PASSES, n], U8, name="xs", tag="xs", bufs=2, align_bytes=64)
+            load_scales(xs, x_scales, slice(starts[blk], starts[blk] + n))
+            staged[blk] = {"xs": xs}
+
+        def stage_codes(blk):
+            n = BLOCKS[blk]
+            xc = work.tile([P, PASSES, 2 * n], U8, name="xc", tag="xc", bufs=2, align_bytes=64)
+            load_codes(xc, x_words, slice(2 * starts[blk], 2 * (starts[blk] + n)))
+            staged[blk]["xc"] = xc
+
+        def stage_freqs(blk):
+            n = BLOCKS[blk]
+            fr = work.tile([P, n // P, HEAD], BF16, name="fr", tag="fr", bufs=2)
+            nc.sync.dma_start(out=fr[:], in_=freqs[starts[blk] : starts[blk] + n, :].rearrange("(t p) d -> p t d", p=P))
+            staged[blk]["fr"] = fr
+
+        def build_tables(blk):
+            nt = BLOCKS[blk] // P
+            pairs = nt * HEAD // 2
+            fr = staged[blk]["fr"][:].rearrange("p t (j e) -> p (t j) e", e=2)
+            cc = work.tile([P, nt, HEAD], BF16, name="cc", tag="cc", bufs=2)
+            sn = work.tile([P, nt, HEAD], BF16, name="sn", tag="sn", bufs=2)
+            ccv = cc[:].rearrange("p t (j e) -> p (t j) e", e=2)
+            snv = sn[:].rearrange("p t (j e) -> p (t j) e", e=2)
+            nc.gpsimd.tensor_scalar(out=ccv, in0=fr[:, :, 0:1].to_broadcast([P, pairs, 2]), scalar1=1.0, scalar2=0.0, op0=ALU.mult, op1=ALU.add)
+            nc.gpsimd.tensor_scalar(out=snv[:, :, 0:1], in0=fr[:, :, 1:2], scalar1=1.0, scalar2=0.0, op0=ALU.mult, op1=ALU.add)
+            nc.gpsimd.tensor_scalar(out=snv[:, :, 1:2], in0=fr[:, :, 1:2], scalar1=-1.0, scalar2=0.0, op0=ALU.mult, op1=ALU.add)
+            staged[blk]["cc"] = cc
+            staged[blk]["sn"] = sn
+
+        eps = keep.tile([P, 1], F32, name="eps")
+        nc.gpsimd.memset(eps[:], EPS)
+        bg_rows = keep.tile([P, P], BF16, name="bg_rows")
+        nc.gpsimd.memset(bg_rows[:], 0.0)
+        nc.scalar.dma_start(out=bg_rows[0:CT, :], in_=b.rearrange("(c p) -> c p", p=P))
+        nc.scalar.dma_start(out=bg_rows[32 : 32 + CT, :], in_=g.rearrange("(c p) -> c p", p=P))
+        warm = keep.tile([P, 1], F32, name="warm")
+        nc.scalar.activation(out=warm[:], in_=eps[:], func=ACT.Sqrt)
+        ident = keep.tile([P, P], F32, name="ident")
+        make_identity(nc, ident[:])
+
+        wc = []
+        ws = []
+        for q in range(CT // GROUP):
+            wcq = keep.tile([P, PASSES, 2 * BANK], U8, name="wc%d" % q, align_bytes=64)
+            wsq = keep.tile([P, PASSES, BANK], U8, name="ws%d" % q, align_bytes=64)
+            wc.append(wcq)
+            ws.append(wsq)
+
+        def load_w_scales(q):
+            load_scales(ws[q], w_scales, slice(BANK * q, BANK * (q + 1)))
+
+        def load_w_codes(q):
+            load_codes(wc[q], w_words, slice(2 * BANK * q, 2 * BANK * (q + 1)))
+
+        load_w_scales(0)
+        stage_scales(0)
+        stage_codes(0)
+        load_w_codes(0)
+        load_w_scales(1)
+        load_w_scales(2)
+        load_w_codes(1)
+        stage_freqs(0)
+        load_w_codes(2)
+        load_w_scales(3)
+        load_w_scales(4)
+        load_w_scales(5)
+        load_w_codes(3)
+        load_w_codes(4)
+        load_w_codes(5)
+        stage_scales(1)
+        stage_codes(1)
+        stage_freqs(1)
+        build_tables(0)
+
+        bg_f32 = keep.tile([P, P], F32, name="bg_f32")
+        nc.vector.tensor_copy(out=bg_f32[:], in_=bg_rows[:])
+        cols = keep.tile([P, P], F32, name="cols")
+        bgcol = keep.tile([P, CT], F32, name="bgcol")
+
+        def turn_bias_and_gain():
+            bank = psum.tile([P, BANK], F32, name="tr", tag="tr")
+            nc.tensor.transpose(out=bank[:, 0:P], in_=bg_f32[:], identity=ident[:])
+            nc.vector.tensor_copy(out=cols[:], in_=bank[:, 0:P])
+            nc.vector.tensor_tensor(out=bgcol[:], in0=cols[:, 0:CT], in1=cols[:, 32 : 32 + CT], op=ALU.mult)
+
+        def project(blk, c):
+            n = BLOCKS[blk]
+            q, j = divmod(c, GROUP)
+            xc = staged[blk]["xc"]
+            xs = staged[blk]["xs"]
+            bank = psum.tile([P, BANK], F32, name="mx", tag="mx")
+            for k in range(PASSES):
+                nc.tensor.matmul_mx(
+                    out=bank[:, 0:n],
+                    lhsT=wc[q][:, k, 2 * P * j : 2 * P * (j + 1)].bitcast(FP4X4),
+                    lhsT_scale=ws[q][:, k, P * j : P * (j + 1)],
+                    rhs=xc[:, k, :].bitcast(FP4X4),
+                    rhs_scale=xs[:, k, :],
+                    start=(k == 0),
+                    stop=(k == PASSES - 1),
+                )
+            return bank
+
+        def evacuate(bank, n, c, acc):
+            u = work.tile([P, n], F32, name="u", tag="u", bufs=8)
+            nc.scalar.activation(out=u[:], in_=bank[:, 0:n], func=ACT.Identity, bias=bgcol[:, c : c + 1], scale=cols[:, 32 + c : 33 + c])
+            if c == 0:
+                nc.scalar.activation(out=acc[:], in_=bank[:, 0:n], func=ACT.Square, bias=cols[:, c : c + 1], scale=1.0)
+            else:
+                sq = work.tile([P, n], F32, name="sq", tag="sq", bufs=3)
+                nc.scalar.activation(out=sq[:], in_=bank[:, 0:n], func=ACT.Square, bias=cols[:, c : c + 1], scale=1.0)
+                nc.gpsimd.tensor_tensor(out=acc[:], in0=acc[:], in1=sq[:], op=ALU.add)
+            return u
+
+        def turn(blk, q, group_u, pend, acc, rstd):
+            nt = BLOCKS[blk] // P
+            cc = staged[blk]["cc"]
+            sn = staged[blk]["sn"]
+            last = q == CT // GROUP - 1
+            if last:
+                sums = psum.tile([P, BANK], F32, name="mx", tag="mx")
+                for t in range(nt):
+                    nc.tensor.transpose(out=sums[:, P * t : P * (t + 1)], in_=acc[:, P * t : P * (t + 1)], identity=ident[:])
+            banks = []
+            for t in range(nt):
+                bank = psum.tile([P, BANK], F32, name="tr", tag="tr")
+                for j in range(GROUP):
+                    nc.tensor.transpose(out=bank[:, P * j : P * (j + 1)], in_=group_u[j][:, P * t : P * (t + 1)], identity=ident[:])
+                banks.append(bank)
+            if last:
+                ssum = work.tile([P, 4], F32, name="ssum", tag="ssum", bufs=2)
+                sdev = work.tile([P, 4], F32, name="sdev", tag="sdev", bufs=2)
+                nc.vector.tensor_reduce(out=ssum[:, 0:nt], in_=sums[:, 0 : P * nt].rearrange("p (t k) -> p t k", k=P), axis=AX.X, op=ALU.add)
+                nc.scalar.activation(out=sdev[:, 0:nt], in_=ssum[:, 0:nt], func=ACT.Sqrt, bias=eps[:], scale=1.0 / DIM)
+            prods = []
+            for t in range(nt):
+                d1 = work.tile([P, BANK], F32, name="d1", tag="d1", bufs=4)
+                p2 = work.tile([P, BANK], F32, name="p2", tag="p2", bufs=4)
+                heads = banks[t][:].rearrange("p (h d) -> p h d", d=HEAD)
+                nc.vector.tensor_tensor(
+                    out=d1[:].rearrange("p (h d) -> p h d", d=HEAD), in0=heads,
+                    in1=cc[:, t, :].unsqueeze(1).to_broadcast([P, BANK // HEAD, HEAD]), op=ALU.mult,
+                )
+                nc.vector.tensor_tensor(
+                    out=p2[:].rearrange("p (h d) -> p h d", d=HEAD), in0=heads,
+                    in1=sn[:, t, :].unsqueeze(1).to_broadcast([P, BANK // HEAD, HEAD]), op=ALU.mult,
+                )
+                prods.append((d1, p2))
+            if last:
+                nc.vector.reciprocal(out=rstd[:, 0:nt], in_=sdev[:, 0:nt])
+            for t in range(nt):
+                d1, p2 = prods[t]
+                nc.vector.tensor_tensor(
+                    out=pend[t][:, BANK * q : BANK * (q + 1)].rearrange("p (n e) -> p n e", e=2),
+                    in0=d1[:].rearrange("p (n e) -> p n e", e=2),
+                    in1=p2[:].rearrange("p (n e) -> p n e", e=2)[:, :, ::-1],
+                    op=ALU.add,
+                )
+
+        def finish(blk, t, half, pend, rstd):
+            r = rstd[:, t : t + 1]
+            a = pend[t][:, BANK * half : BANK * (half + 1)]
+            bb = pend[t][:, BANK * (2 + half) : BANK * (3 + half)]
+            cv = pend[t][:, BANK * (4 + half) : BANK * (5 + half)]
+            nc.scalar.activation(out=a, in_=a, func=ACT.Copy, scale=r)
+            nc.gpsimd.tensor_scalar(out=bb, in0=bb, scalar1=r, scalar2=0.0, op0=ALU.mult, op1=ALU.add)
+            nc.vector.tensor_scalar_mul(out=cv, in0=cv, scalar1=r)
+            if half == 1:
+                row0 = starts[blk] + P * t
+                nc.sync.dma_start(out=out_rows[row0 : row0 + P, :], in_=pend[t][:])
+
+        turns = []
+        finishes = []
+        cursor = {"turn": 0, "finish": 0, "due": 0}
+
+        def run_due(now, everything):
+            while cursor["turn"] < len(turns) and (everything or turns[cursor["turn"]][0] <= now):
+                turns[cursor["turn"]][1]()
+                cursor["turn"] += 1
+            while cursor["finish"] < len(finishes) and (everything or finishes[cursor["finish"]][0] <= now):
+                finishes[cursor["finish"]][1]()
+                cursor["finish"] += 1
+                if not everything:
+                    break
+
+        now = 0
+        for blk, n in enumerate(BLOCKS):
+            nt = n // P
+            pend = [work.tile([P, DIM], F32, name="pend", tag="pend", bufs=8) for t in range(nt)]
+            acc = work.tile([P, n], F32, name="acc", tag="acc", bufs=2)
+            rstd = work.tile([P, 4], F32, name="rstd", tag="rstd", bufs=3)
+            group_u = []
+            for c in range(CT):
+                if c == 0 and 1 <= blk < len(BLOCKS) - 1:
+                    stage_scales(blk + 1)
+                    stage_codes(blk + 1)
+                    stage_freqs(blk + 1)
+                if c == CT // 2 and blk < len(BLOCKS) - 1:
+                    build_tables(blk + 1)
+                bank = project(blk, c)
+                if blk == 0 and c == 0:
+                    turn_bias_and_gain()
+                group_u.append(evacuate(bank, n, c, acc))
+                now += n
+                if c % GROUP == GROUP - 1:
+                    turns.append([now + TURN_LAG * n, lambda blk=blk, q=c // GROUP, gu=group_u, pend=pend, acc=acc, rstd=rstd: turn(blk, q, gu, pend, acc, rstd)])
+                    group_u = []
+                run_due(now, False)
+            for t in range(nt):
+                for half in range(2):
+                    cursor["due"] = max(now + FINISH_LAG * n, cursor["due"] + FINISH_STEP)
+                    finishes.append([cursor["due"], lambda blk=blk, t=t, half=half, pend=pend, rstd=rstd: finish(blk, t, half, pend, rstd)])
+        run_due(now, True)

@@ -20,11 +20,15 @@ P = 128
 PASSES = DIM // 512
 CT = DIM // P
 GROUP = 4
+NGROUPS = CT // GROUP
 BANK = 512
-BLOCKS = (512, 512, 512, 256, 128, 128)
+BLOCKS = (512, 512, 512, 256, 256)
 TURN_LAG = 2
+NORM_LAG = 6
 FINISH_LAG = 7
 FINISH_STEP = 512
+ACT_W = 1024
+POOL_SHARE = 3
 
 
 def tile_causalwanselfattention_pa_kernel(tc, x_words, x_scales, w_words, w_scales, b, g, freqs, out):
@@ -37,25 +41,27 @@ def tile_causalwanselfattention_pa_kernel(tc, x_words, x_scales, w_words, w_scal
         psum = ctx.enter_context(tc.psum_pool(name="psum", bufs=4))
         ctx.enter_context(tc.manual_schedule())
 
-        def load_scales(plane, src, cols):
+        def load_scales(plane, src, span):
             nc.vector.memset(plane[:].bitcast(I32), 0)
             for quad in range(4):
                 nc.sync.dma_start(
                     out=plane[32 * quad : 32 * quad + 4, :, :].bitcast(I32),
-                    in_=src[:, 4 * quad : 4 * quad + 4, cols].rearrange("k r n -> r k n").bitcast(I32),
+                    in_=src[:, 4 * quad : 4 * quad + 4, span].rearrange("k r n -> r k n").bitcast(I32),
                 )
 
-        def load_codes(codes, src, cols):
-            nc.sync.dma_start(out=codes[:].bitcast(I32), in_=src[:, :, cols].rearrange("k p n -> p k n").bitcast(I32))
+        def load_codes(codes, src, span):
+            nc.sync.dma_start(out=codes[:].bitcast(I32), in_=src[:, :, span].rearrange("k p n -> p k n").bitcast(I32))
 
         starts = [sum(BLOCKS[:i]) for i in range(len(BLOCKS))]
         staged = {}
+        for blk in range(len(BLOCKS)):
+            staged[blk] = {}
 
         def stage_scales(blk):
             n = BLOCKS[blk]
             xs = work.tile([P, PASSES, n], U8, name="xs", tag="xs", bufs=2, align_bytes=64)
             load_scales(xs, x_scales, slice(starts[blk], starts[blk] + n))
-            staged[blk] = {"xs": xs}
+            staged[blk]["xs"] = xs
 
         def stage_codes(blk):
             n = BLOCKS[blk]
@@ -69,7 +75,7 @@ def tile_causalwanselfattention_pa_kernel(tc, x_words, x_scales, w_words, w_scal
             nc.sync.dma_start(out=fr[:], in_=freqs[starts[blk] : starts[blk] + n, :].rearrange("(t p) d -> p t d", p=P))
             staged[blk]["fr"] = fr
 
-        def build_tables(blk):
+        def table_steps(blk):
             nt = BLOCKS[blk] // P
             pairs = nt * HEAD // 2
             fr = staged[blk]["fr"][:].rearrange("p t (j e) -> p (t j) e", e=2)
@@ -77,26 +83,17 @@ def tile_causalwanselfattention_pa_kernel(tc, x_words, x_scales, w_words, w_scal
             sn = work.tile([P, nt, HEAD], BF16, name="sn", tag="sn", bufs=2)
             ccv = cc[:].rearrange("p t (j e) -> p (t j) e", e=2)
             snv = sn[:].rearrange("p t (j e) -> p (t j) e", e=2)
-            nc.gpsimd.tensor_scalar(out=ccv, in0=fr[:, :, 0:1].to_broadcast([P, pairs, 2]), scalar1=1.0, scalar2=0.0, op0=ALU.mult, op1=ALU.add)
-            nc.gpsimd.tensor_scalar(out=snv[:, :, 0:1], in0=fr[:, :, 1:2], scalar1=1.0, scalar2=0.0, op0=ALU.mult, op1=ALU.add)
-            nc.gpsimd.tensor_scalar(out=snv[:, :, 1:2], in0=fr[:, :, 1:2], scalar1=-1.0, scalar2=0.0, op0=ALU.mult, op1=ALU.add)
             staged[blk]["cc"] = cc
             staged[blk]["sn"] = sn
-
-        eps = keep.tile([P, 1], F32, name="eps")
-        nc.gpsimd.memset(eps[:], EPS)
-        bg_rows = keep.tile([P, P], BF16, name="bg_rows")
-        nc.gpsimd.memset(bg_rows[:], 0.0)
-        nc.scalar.dma_start(out=bg_rows[0:CT, :], in_=b.rearrange("(c p) -> c p", p=P))
-        nc.scalar.dma_start(out=bg_rows[32 : 32 + CT, :], in_=g.rearrange("(c p) -> c p", p=P))
-        warm = keep.tile([P, 1], F32, name="warm")
-        nc.scalar.activation(out=warm[:], in_=eps[:], func=ACT.Sqrt)
-        ident = keep.tile([P, P], F32, name="ident")
-        make_identity(nc, ident[:])
+            return [
+                lambda: nc.gpsimd.tensor_scalar(out=ccv, in0=fr[:, :, 0:1].to_broadcast([P, pairs, 2]), scalar1=1.0, scalar2=0.0, op0=ALU.mult, op1=ALU.add),
+                lambda: nc.gpsimd.tensor_scalar(out=snv[:, :, 0:1], in0=fr[:, :, 1:2], scalar1=1.0, scalar2=0.0, op0=ALU.mult, op1=ALU.add),
+                lambda: nc.gpsimd.tensor_scalar(out=snv[:, :, 1:2], in0=fr[:, :, 1:2], scalar1=-1.0, scalar2=0.0, op0=ALU.mult, op1=ALU.add),
+            ]
 
         wc = []
         ws = []
-        for q in range(CT // GROUP):
+        for q in range(NGROUPS):
             wcq = keep.tile([P, PASSES, 2 * BANK], U8, name="wc%d" % q, align_bytes=64)
             wsq = keep.tile([P, PASSES, BANK], U8, name="ws%d" % q, align_bytes=64)
             wc.append(wcq)
@@ -108,10 +105,21 @@ def tile_causalwanselfattention_pa_kernel(tc, x_words, x_scales, w_words, w_scal
         def load_w_codes(q):
             load_codes(wc[q], w_words, slice(2 * BANK * q, 2 * BANK * (q + 1)))
 
-        load_w_scales(0)
-        stage_scales(0)
+        eps = keep.tile([P, 1], F32, name="eps")
+        nc.gpsimd.memset(eps[:], EPS)
+        bg_rows = keep.tile([P, P], BF16, name="bg_rows")
+        nc.gpsimd.memset(bg_rows[:], 0.0)
+        ident = keep.tile([P, P], F32, name="ident")
+        make_identity(nc, ident[:])
+        warm = keep.tile([P, 1], F32, name="warm")
+        nc.scalar.activation(out=warm[:], in_=eps[:], func=ACT.Sqrt)
+
         stage_codes(0)
         load_w_codes(0)
+        load_w_scales(0)
+        stage_scales(0)
+        nc.scalar.dma_start(out=bg_rows[0:CT, :], in_=b.rearrange("(c p) -> c p", p=P))
+        nc.scalar.dma_start(out=bg_rows[32 : 32 + CT, :], in_=g.rearrange("(c p) -> c p", p=P))
         load_w_scales(1)
         load_w_scales(2)
         load_w_codes(1)
@@ -126,18 +134,23 @@ def tile_causalwanselfattention_pa_kernel(tc, x_words, x_scales, w_words, w_scal
         stage_scales(1)
         stage_codes(1)
         stage_freqs(1)
-        build_tables(0)
+        for step in table_steps(0):
+            step()
 
         bg_f32 = keep.tile([P, P], F32, name="bg_f32")
         nc.vector.tensor_copy(out=bg_f32[:], in_=bg_rows[:])
         cols = keep.tile([P, P], F32, name="cols")
         bgcol = keep.tile([P, CT], F32, name="bgcol")
+        flag = keep.tile([P, 1], F32, name="flag")
 
         def turn_bias_and_gain():
             bank = psum.tile([P, BANK], F32, name="tr", tag="tr")
             nc.tensor.transpose(out=bank[:, 0:P], in_=bg_f32[:], identity=ident[:])
             nc.vector.tensor_copy(out=cols[:], in_=bank[:, 0:P])
             nc.vector.tensor_tensor(out=bgcol[:], in0=cols[:, 0:CT], in1=cols[:, 32 : 32 + CT], op=ALU.mult)
+
+        owed = []
+        chores = []
 
         def project(blk, c):
             n = BLOCKS[blk]
@@ -163,20 +176,19 @@ def tile_causalwanselfattention_pa_kernel(tc, x_words, x_scales, w_words, w_scal
             if c == 0:
                 nc.scalar.activation(out=acc[:], in_=bank[:, 0:n], func=ACT.Square, bias=cols[:, c : c + 1], scale=1.0)
             else:
-                sq = work.tile([P, n], F32, name="sq", tag="sq", bufs=3)
+                sq = work.tile([P, n], F32, name="sq", tag="sq", bufs=6)
                 nc.scalar.activation(out=sq[:], in_=bank[:, 0:n], func=ACT.Square, bias=cols[:, c : c + 1], scale=1.0)
-                nc.gpsimd.tensor_tensor(out=acc[:], in0=acc[:], in1=sq[:], op=ALU.add)
+                if c >= CT - TURN_LAG:
+                    nc.vector.tensor_tensor(out=acc[:], in0=acc[:], in1=sq[:], op=ALU.add)
+                else:
+                    owed.append((acc, sq))
             return u
 
-        def turn(blk, q, group_u, pend, acc, rstd):
+        def turn(blk, q, group_u, pend, acc, ssum):
             nt = BLOCKS[blk] // P
             cc = staged[blk]["cc"]
             sn = staged[blk]["sn"]
-            last = q == CT // GROUP - 1
-            if last:
-                sums = psum.tile([P, BANK], F32, name="mx", tag="mx")
-                for t in range(nt):
-                    nc.tensor.transpose(out=sums[:, P * t : P * (t + 1)], in_=acc[:, P * t : P * (t + 1)], identity=ident[:])
+            last = q == NGROUPS - 1
             banks = []
             for t in range(nt):
                 bank = psum.tile([P, BANK], F32, name="tr", tag="tr")
@@ -184,10 +196,18 @@ def tile_causalwanselfattention_pa_kernel(tc, x_words, x_scales, w_words, w_scal
                     nc.tensor.transpose(out=bank[:, P * j : P * (j + 1)], in_=group_u[j][:, P * t : P * (t + 1)], identity=ident[:])
                 banks.append(bank)
             if last:
-                ssum = work.tile([P, 4], F32, name="ssum", tag="ssum", bufs=2)
-                sdev = work.tile([P, 4], F32, name="sdev", tag="sdev", bufs=2)
-                nc.vector.tensor_reduce(out=ssum[:, 0:nt], in_=sums[:, 0 : P * nt].rearrange("p (t k) -> p t k", k=P), axis=AX.X, op=ALU.add)
-                nc.scalar.activation(out=sdev[:, 0:nt], in_=ssum[:, 0:nt], func=ACT.Sqrt, bias=eps[:], scale=1.0 / DIM)
+                sums = psum.tile([P, BANK], F32, name="mx", tag="mx")
+                for t in range(nt):
+                    nc.tensor.transpose(out=sums[:, P * t : P * (t + 1)], in_=acc[:, P * t : P * (t + 1)], identity=ident[:])
+            mine = list(owed)
+            owed.clear()
+            if mine:
+                nc.vector.tensor_copy(out=flag[:], in_=mine[0][0][:, 0:1])
+            for a, sq in mine[:POOL_SHARE]:
+                nc.gpsimd.tensor_tensor(out=a[:], in0=a[:], in1=sq[:], op=ALU.add)
+            if chores:
+                chores[0]()
+                chores.remove(chores[0])
             prods = []
             for t in range(nt):
                 d1 = work.tile([P, BANK], F32, name="d1", tag="d1", bufs=4)
@@ -203,47 +223,62 @@ def tile_causalwanselfattention_pa_kernel(tc, x_words, x_scales, w_words, w_scal
                 )
                 prods.append((d1, p2))
             if last:
-                nc.vector.reciprocal(out=rstd[:, 0:nt], in_=sdev[:, 0:nt])
-            for t in range(nt):
-                d1, p2 = prods[t]
-                nc.vector.tensor_tensor(
-                    out=pend[t][:, BANK * q : BANK * (q + 1)].rearrange("p (n e) -> p n e", e=2),
-                    in0=d1[:].rearrange("p (n e) -> p n e", e=2),
-                    in1=p2[:].rearrange("p (n e) -> p n e", e=2)[:, :, ::-1],
-                    op=ALU.add,
-                )
+                nc.vector.tensor_reduce(out=ssum[:, 0:nt], in_=sums[:, 0 : P * nt].rearrange("p (t k) -> p t k", k=P), axis=AX.X, op=ALU.add)
+            rest = mine[POOL_SHARE:]
+            for t in range(max(nt, len(rest))):
+                if t < nt:
+                    d1, p2 = prods[t]
+                    nc.vector.tensor_tensor(
+                        out=pend[t][:, BANK * q : BANK * (q + 1)].rearrange("p (n e) -> p n e", e=2),
+                        in0=d1[:].rearrange("p (n e) -> p n e", e=2),
+                        in1=p2[:].rearrange("p (n e) -> p n e", e=2)[:, :, ::-1],
+                        op=ALU.add,
+                    )
+                if t < len(rest):
+                    a, sq = rest[t]
+                    nc.vector.tensor_tensor(out=a[:], in0=a[:], in1=sq[:], op=ALU.add)
+
+        def norm(nt, ssum, rstd):
+            sdev = work.tile([P, 4], F32, name="sdev", tag="sdev", bufs=2)
+            nc.scalar.activation(out=sdev[:, 0:nt], in_=ssum[:, 0:nt], func=ACT.Sqrt, bias=eps[:], scale=1.0 / DIM)
+            nc.vector.reciprocal(out=rstd[:, 0:nt], in_=sdev[:, 0:nt])
 
         def finish(blk, t, half, pend, rstd):
             r = rstd[:, t : t + 1]
-            a = pend[t][:, BANK * half : BANK * (half + 1)]
-            bb = pend[t][:, BANK * (2 + half) : BANK * (3 + half)]
-            cv = pend[t][:, BANK * (4 + half) : BANK * (5 + half)]
-            nc.scalar.activation(out=a, in_=a, func=ACT.Copy, scale=r)
-            nc.gpsimd.tensor_scalar(out=bb, in0=bb, scalar1=r, scalar2=0.0, op0=ALU.mult, op1=ALU.add)
-            nc.vector.tensor_scalar_mul(out=cv, in0=cv, scalar1=r)
-            if half == 1:
-                row0 = starts[blk] + P * t
+            row0 = starts[blk] + P * t
+            tail = blk == len(BLOCKS) - 1
+            act_w = 512 if tail else ACT_W
+            dve_w = DIM // 2 - act_w
+            a0 = act_w * half
+            v0 = 2 * act_w + dve_w * half
+            nc.scalar.activation(out=pend[t][:, a0 : a0 + act_w], in_=pend[t][:, a0 : a0 + act_w], func=ACT.Copy, scale=r)
+            if dve_w:
+                nc.vector.tensor_scalar_mul(out=pend[t][:, v0 : v0 + dve_w], in0=pend[t][:, v0 : v0 + dve_w], scalar1=r)
+            if tail:
+                nc.sync.dma_start(out=out_rows[row0 : row0 + P, v0 : v0 + dve_w], in_=pend[t][:, v0 : v0 + dve_w])
+                nc.sync.dma_start(out=out_rows[row0 : row0 + P, a0 : a0 + act_w], in_=pend[t][:, a0 : a0 + act_w])
+            elif half == 1:
                 nc.sync.dma_start(out=out_rows[row0 : row0 + P, :], in_=pend[t][:])
 
-        turns = []
-        finishes = []
-        cursor = {"turn": 0, "finish": 0, "due": 0}
+        todo = []
+        state = {"serial": 0, "due": 0}
+
+        def later(due, fn):
+            todo.append([due, state["serial"], fn])
+            state["serial"] += 1
 
         def run_due(now, everything):
-            while cursor["turn"] < len(turns) and (everything or turns[cursor["turn"]][0] <= now):
-                turns[cursor["turn"]][1]()
-                cursor["turn"] += 1
-            while cursor["finish"] < len(finishes) and (everything or finishes[cursor["finish"]][0] <= now):
-                finishes[cursor["finish"]][1]()
-                cursor["finish"] += 1
-                if not everything:
-                    break
+            ready = [e for e in todo if everything or e[0] <= now]
+            for e in sorted(ready, key=lambda e: (e[0], e[1])):
+                e[2]()
+                todo.remove(e)
 
         now = 0
         for blk, n in enumerate(BLOCKS):
             nt = n // P
             pend = [work.tile([P, DIM], F32, name="pend", tag="pend", bufs=8) for t in range(nt)]
             acc = work.tile([P, n], F32, name="acc", tag="acc", bufs=2)
+            ssum = work.tile([P, 4], F32, name="ssum", tag="ssum", bufs=2)
             rstd = work.tile([P, 4], F32, name="rstd", tag="rstd", bufs=3)
             group_u = []
             for c in range(CT):
@@ -251,19 +286,20 @@ def tile_causalwanselfattention_pa_kernel(tc, x_words, x_scales, w_words, w_scal
                     stage_scales(blk + 1)
                     stage_codes(blk + 1)
                     stage_freqs(blk + 1)
-                if c == CT // 2 and blk < len(BLOCKS) - 1:
-                    build_tables(blk + 1)
+                if c == GROUP and blk < len(BLOCKS) - 1:
+                    chores.extend(table_steps(blk + 1))
                 bank = project(blk, c)
                 if blk == 0 and c == 0:
                     turn_bias_and_gain()
                 group_u.append(evacuate(bank, n, c, acc))
                 now += n
                 if c % GROUP == GROUP - 1:
-                    turns.append([now + TURN_LAG * n, lambda blk=blk, q=c // GROUP, gu=group_u, pend=pend, acc=acc, rstd=rstd: turn(blk, q, gu, pend, acc, rstd)])
+                    later(now + TURN_LAG * n, lambda blk=blk, q=c // GROUP, gu=group_u, pend=pend, acc=acc, ssum=ssum: turn(blk, q, gu, pend, acc, ssum))
                     group_u = []
                 run_due(now, False)
+            later(now + NORM_LAG * n, lambda nt=nt, ssum=ssum, rstd=rstd: norm(nt, ssum, rstd))
             for t in range(nt):
                 for half in range(2):
-                    cursor["due"] = max(now + FINISH_LAG * n, cursor["due"] + FINISH_STEP)
-                    finishes.append([cursor["due"], lambda blk=blk, t=t, half=half, pend=pend, rstd=rstd: finish(blk, t, half, pend, rstd)])
+                    state["due"] = max(now + FINISH_LAG * n, state["due"] + FINISH_STEP)
+                    later(state["due"], lambda blk=blk, t=t, half=half, pend=pend, rstd=rstd: finish(blk, t, half, pend, rstd))
         run_due(now, True)

@@ -19,21 +19,20 @@ AX = mybir.AxisListType
 P = 128
 PASSES = DIM // 512
 CT = DIM // P
-GROUP = 4
-NGROUPS = CT // GROUP
 BANK = 512
-BLOCKS = (512, 512, 512, 256, 256)
+QUARTERS = BANK // P
+BLOCKS = (512, 512, 512, 256, 128, 128)
+LAST_GROUPS = {128: (3, 2, 1), 256: (4, 4, 2, 2), 512: (4, 4, 4, 4, 4, 4)}
 TURN_LAG = 2
-NORM_LAG = 6
-FINISH_LAG = 7
-FINISH_STEP = 512
 ACT_W = 1024
-POOL_SHARE = 3
+PARTS = 2
+ALL_ACT_FROM = 4
 
 
 def tile_causalwanselfattention_pa_kernel(tc, x_words, x_scales, w_words, w_scales, b, g, freqs, out):
     nc = tc.nc
     out_rows = out.rearrange("r h d -> r (h d)")
+    final_blk = len(BLOCKS) - 1
 
     with ExitStack() as ctx:
         keep = ctx.enter_context(tc.tile_pool(name="keep", bufs=1))
@@ -71,29 +70,28 @@ def tile_causalwanselfattention_pa_kernel(tc, x_words, x_scales, w_words, w_scal
 
         def stage_freqs(blk):
             n = BLOCKS[blk]
-            fr = work.tile([P, n // P, HEAD], BF16, name="fr", tag="fr", bufs=2)
-            nc.sync.dma_start(out=fr[:], in_=freqs[starts[blk] : starts[blk] + n, :].rearrange("(t p) d -> p t d", p=P))
+            fr = work.tile([P, n // P, HEAD], BF16, name="fr", tag="fr", bufs=3)
+            nc.gpsimd.dma_start(out=fr[:], in_=freqs[starts[blk] : starts[blk] + n, :].rearrange("(t p) d -> p t d", p=P))
             staged[blk]["fr"] = fr
 
         def table_steps(blk):
             nt = BLOCKS[blk] // P
             pairs = nt * HEAD // 2
             fr = staged[blk]["fr"][:].rearrange("p t (j e) -> p (t j) e", e=2)
-            cc = work.tile([P, nt, HEAD], BF16, name="cc", tag="cc", bufs=2)
-            sn = work.tile([P, nt, HEAD], BF16, name="sn", tag="sn", bufs=2)
-            ccv = cc[:].rearrange("p t (j e) -> p (t j) e", e=2)
-            snv = sn[:].rearrange("p t (j e) -> p (t j) e", e=2)
-            staged[blk]["cc"] = cc
-            staged[blk]["sn"] = sn
+            tab = work.tile([P, 2, nt, HEAD], BF16, name="tab", tag="tab", bufs=2)
+            ccv = tab[:, 0, :, :].rearrange("p t (j e) -> p (t j) e", e=2)
+            snv = tab[:, 1, :, :].rearrange("p t (j e) -> p (t j) e", e=2)
+            staged[blk]["tab"] = tab
+
             return [
-                lambda: nc.gpsimd.tensor_scalar(out=ccv, in0=fr[:, :, 0:1].to_broadcast([P, pairs, 2]), scalar1=1.0, scalar2=0.0, op0=ALU.mult, op1=ALU.add),
-                lambda: nc.gpsimd.tensor_scalar(out=snv[:, :, 0:1], in0=fr[:, :, 1:2], scalar1=1.0, scalar2=0.0, op0=ALU.mult, op1=ALU.add),
-                lambda: nc.gpsimd.tensor_scalar(out=snv[:, :, 1:2], in0=fr[:, :, 1:2], scalar1=-1.0, scalar2=0.0, op0=ALU.mult, op1=ALU.add),
+                lambda: nc.scalar.activation(out=ccv, in_=fr[:, :, 0:1].to_broadcast([P, pairs, 2]), func=ACT.Copy),
+                lambda: nc.scalar.activation(out=snv[:, :, 0:1], in_=fr[:, :, 1:2], func=ACT.Copy),
+                lambda: nc.scalar.activation(out=snv[:, :, 1:2], in_=fr[:, :, 1:2], func=ACT.Copy, scale=-1.0),
             ]
 
         wc = []
         ws = []
-        for q in range(NGROUPS):
+        for q in range(CT // QUARTERS):
             wcq = keep.tile([P, PASSES, 2 * BANK], U8, name="wc%d" % q, align_bytes=64)
             wsq = keep.tile([P, PASSES, BANK], U8, name="ws%d" % q, align_bytes=64)
             wc.append(wcq)
@@ -114,6 +112,9 @@ def tile_causalwanselfattention_pa_kernel(tc, x_words, x_scales, w_words, w_scal
         warm = keep.tile([P, 1], F32, name="warm")
         nc.scalar.activation(out=warm[:], in_=eps[:], func=ACT.Sqrt)
 
+        stage_freqs(0)
+        stage_freqs(1)
+        stage_freqs(2)
         stage_codes(0)
         load_w_codes(0)
         load_w_scales(0)
@@ -123,7 +124,6 @@ def tile_causalwanselfattention_pa_kernel(tc, x_words, x_scales, w_words, w_scal
         load_w_scales(1)
         load_w_scales(2)
         load_w_codes(1)
-        stage_freqs(0)
         load_w_codes(2)
         load_w_scales(3)
         load_w_scales(4)
@@ -133,7 +133,6 @@ def tile_causalwanselfattention_pa_kernel(tc, x_words, x_scales, w_words, w_scal
         load_w_codes(5)
         stage_scales(1)
         stage_codes(1)
-        stage_freqs(1)
         for step in table_steps(0):
             step()
 
@@ -152,113 +151,147 @@ def tile_causalwanselfattention_pa_kernel(tc, x_words, x_scales, w_words, w_scal
         owed = []
         chores = []
 
-        def project(blk, c):
+        def project(blk, s):
             n = BLOCKS[blk]
-            q, j = divmod(c, GROUP)
             xc = staged[blk]["xc"]
             xs = staged[blk]["xs"]
             bank = psum.tile([P, BANK], F32, name="mx", tag="mx")
-            for k in range(PASSES):
-                nc.tensor.matmul_mx(
-                    out=bank[:, 0:n],
-                    lhsT=wc[q][:, k, 2 * P * j : 2 * P * (j + 1)].bitcast(FP4X4),
-                    lhsT_scale=ws[q][:, k, P * j : P * (j + 1)],
-                    rhs=xc[:, k, :].bitcast(FP4X4),
-                    rhs_scale=xs[:, k, :],
-                    start=(k == 0),
-                    stop=(k == PASSES - 1),
-                )
+            for j in range(BANK // n):
+                q, i = divmod(s * (BANK // n) + j, QUARTERS)
+                for k in range(PASSES):
+                    nc.tensor.matmul_mx(
+                        out=bank[:, n * j : n * (j + 1)],
+                        lhsT=wc[q][:, k, 2 * P * i : 2 * P * (i + 1)].bitcast(FP4X4),
+                        lhsT_scale=ws[q][:, k, P * i : P * (i + 1)],
+                        rhs=xc[:, k, :].bitcast(FP4X4),
+                        rhs_scale=xs[:, k, :],
+                        start=(k == 0),
+                        stop=(k == PASSES - 1),
+                    )
             return bank
 
-        def evacuate(bank, n, c, acc):
-            u = work.tile([P, n], F32, name="u", tag="u", bufs=8)
-            nc.scalar.activation(out=u[:], in_=bank[:, 0:n], func=ACT.Identity, bias=bgcol[:, c : c + 1], scale=cols[:, 32 + c : 33 + c])
-            if c == 0:
-                nc.scalar.activation(out=acc[:], in_=bank[:, 0:n], func=ACT.Square, bias=cols[:, c : c + 1], scale=1.0)
-            else:
-                sq = work.tile([P, n], F32, name="sq", tag="sq", bufs=6)
-                nc.scalar.activation(out=sq[:], in_=bank[:, 0:n], func=ACT.Square, bias=cols[:, c : c + 1], scale=1.0)
-                if c >= CT - TURN_LAG:
-                    nc.vector.tensor_tensor(out=acc[:], in0=acc[:], in1=sq[:], op=ALU.add)
-                else:
-                    owed.append((acc, sq))
+        def evacuate(bank, blk, s, acc, at_once):
+            n = BLOCKS[blk]
+            u = work.tile([P, BANK], F32, name="u", tag="u", bufs=8)
+            sq = acc
+            if s > 0:
+                sq = work.tile([P, BANK], F32, name="sq", tag="sq", bufs=6)
+            for j in range(BANK // n):
+                c = s * (BANK // n) + j
+                span = slice(n * j, n * (j + 1))
+                nc.scalar.activation(out=u[:, span], in_=bank[:, span], func=ACT.Identity, bias=bgcol[:, c : c + 1], scale=cols[:, 32 + c : 33 + c])
+            for j in range(BANK // n):
+                c = s * (BANK // n) + j
+                span = slice(n * j, n * (j + 1))
+                nc.scalar.activation(out=sq[:, span], in_=bank[:, span], func=ACT.Square, bias=cols[:, c : c + 1], scale=1.0)
+            if s > 0 and at_once:
+                nc.vector.tensor_tensor(out=acc[:], in0=acc[:], in1=sq[:], op=ALU.add)
+            elif s > 0:
+                owed.append((acc, sq))
             return u
 
-        def turn(blk, q, group_u, pend, acc, ssum):
-            nt = BLOCKS[blk] // P
-            cc = staged[blk]["cc"]
-            sn = staged[blk]["sn"]
-            last = q == NGROUPS - 1
+        def turn_to_tokens(blk, c0, group_u, closing, acc, ssum, sdev, carry):
+            n = BLOCKS[blk]
+            nt = n // P
+            per_slot = BANK // n
+            tab = staged[blk]["tab"]
+            tail = closing and blk == final_blk
             banks = []
-            for t in range(nt):
-                bank = psum.tile([P, BANK], F32, name="tr", tag="tr")
-                for j in range(GROUP):
-                    nc.tensor.transpose(out=bank[:, P * j : P * (j + 1)], in_=group_u[j][:, P * t : P * (t + 1)], identity=ident[:])
-                banks.append(bank)
-            if last:
-                sums = psum.tile([P, BANK], F32, name="mx", tag="mx")
+            for m in range(len(group_u) * per_slot // QUARTERS):
                 for t in range(nt):
-                    nc.tensor.transpose(out=sums[:, P * t : P * (t + 1)], in_=acc[:, P * t : P * (t + 1)], identity=ident[:])
+                    bank = psum.tile([P, BANK], F32, name="tr", tag="tr")
+                    for i in range(QUARTERS):
+                        si, j = divmod(QUARTERS * m + i, per_slot)
+                        nc.tensor.transpose(out=bank[:, P * i : P * (i + 1)], in_=group_u[si][:, n * j + P * t : n * j + P * (t + 1)], identity=ident[:])
+                    banks.append((bank, t))
+
+            def sum_of_squares():
+                sums = psum.tile([P, BANK], F32, name="mx", tag="mx")
+                for i in range(QUARTERS):
+                    nc.tensor.transpose(out=sums[:, P * i : P * (i + 1)], in_=acc[:, P * i : P * (i + 1)], identity=ident[:])
+                junk = work.tile([P, BANK], F32, name="junk", tag="junk", bufs=1)
+                by_token = sums[:].rearrange("p (j t k) -> p t j k", t=nt, k=P)
+                for t in range(nt):
+                    nc.scalar.activation(
+                        out=junk[:, per_slot * P * t : per_slot * P * (t + 1)].rearrange("p (j k) -> p j k", k=P),
+                        in_=by_token[:, t, :, :], func=ACT.Copy, accum_out=ssum[:, t : t + 1],
+                    )
+                nc.scalar.activation(out=sdev[:, 0:nt], in_=ssum[:, 0:nt], func=ACT.Sqrt, bias=eps[:], scale=1.0 / DIM)
+
+            if closing and not tail:
+                sum_of_squares()
             mine = list(owed)
             owed.clear()
-            if mine:
+            room = 0 if tail else len(banks) - 1
+            if mine and room:
                 nc.vector.tensor_copy(out=flag[:], in_=mine[0][0][:, 0:1])
-            for a, sq in mine[:POOL_SHARE]:
+            for a, sq in mine[:room]:
                 nc.gpsimd.tensor_tensor(out=a[:], in0=a[:], in1=sq[:], op=ALU.add)
-            if chores:
-                chores[0]()
-                chores.remove(chores[0])
-            prods = []
-            for t in range(nt):
-                d1 = work.tile([P, BANK], F32, name="d1", tag="d1", bufs=4)
-                p2 = work.tile([P, BANK], F32, name="p2", tag="p2", bufs=4)
-                heads = banks[t][:].rearrange("p (h d) -> p h d", d=HEAD)
+            rest = mine[room:]
+            prods = work.tile([P, QUARTERS, 2, BANK], F32, name="prods", tag="prods", bufs=1)
+            for i in range(len(banks)):
+                bank, t = banks[i]
                 nc.vector.tensor_tensor(
-                    out=d1[:].rearrange("p (h d) -> p h d", d=HEAD), in0=heads,
-                    in1=cc[:, t, :].unsqueeze(1).to_broadcast([P, BANK // HEAD, HEAD]), op=ALU.mult,
+                    out=prods[:, i, :, :].rearrange("p a (h d) -> p a h d", d=HEAD),
+                    in0=bank[:].unsqueeze(1).to_broadcast([P, 2, BANK]).rearrange("p a (h d) -> p a h d", d=HEAD),
+                    in1=tab[:, :, t, :].unsqueeze(2).to_broadcast([P, 2, BANK // HEAD, HEAD]),
+                    op=ALU.mult,
                 )
+            if tail:
+                for a, sq in rest:
+                    nc.vector.tensor_tensor(out=a[:], in0=a[:], in1=sq[:], op=ALU.add)
+                rest = []
+                sum_of_squares()
+            carry["rest"] = rest
+            carry["prods"] = prods
+            carry["banks"] = len(banks)
+
+        def rotate(blk, c0, closing, pend, sdev, rstd, carry):
+            nt = BLOCKS[blk] // P
+            t0 = starts[blk] % BANK // P
+            prods = carry["prods"]
+            for a, sq in carry["rest"]:
+                nc.vector.tensor_tensor(out=a[:], in0=a[:], in1=sq[:], op=ALU.add)
+            chunk0 = c0 // QUARTERS
+            if nt == 1:
+                k = carry["banks"]
                 nc.vector.tensor_tensor(
-                    out=p2[:].rearrange("p (h d) -> p h d", d=HEAD), in0=heads,
-                    in1=sn[:, t, :].unsqueeze(1).to_broadcast([P, BANK // HEAD, HEAD]), op=ALU.mult,
+                    out=pend[:, t0, BANK * chunk0 : BANK * (chunk0 + k)].rearrange("p (m n e) -> p m n e", m=k, e=2),
+                    in0=prods[:, 0:k, 0, :].rearrange("p m (n e) -> p m n e", e=2),
+                    in1=prods[:, 0:k, 1, :].rearrange("p m (n e) -> p m n e", e=2)[:, :, :, ::-1],
+                    op=ALU.add,
                 )
-                prods.append((d1, p2))
-            if last:
-                nc.vector.tensor_reduce(out=ssum[:, 0:nt], in_=sums[:, 0 : P * nt].rearrange("p (t k) -> p t k", k=P), axis=AX.X, op=ALU.add)
-            rest = mine[POOL_SHARE:]
-            for t in range(max(nt, len(rest))):
-                if t < nt:
-                    d1, p2 = prods[t]
+            else:
+                for m in range(carry["banks"] // nt):
                     nc.vector.tensor_tensor(
-                        out=pend[t][:, BANK * q : BANK * (q + 1)].rearrange("p (n e) -> p n e", e=2),
-                        in0=d1[:].rearrange("p (n e) -> p n e", e=2),
-                        in1=p2[:].rearrange("p (n e) -> p n e", e=2)[:, :, ::-1],
+                        out=pend[:, t0 : t0 + nt, BANK * (chunk0 + m) : BANK * (chunk0 + m + 1)].rearrange("p t (n e) -> p t n e", e=2),
+                        in0=prods[:, nt * m : nt * (m + 1), 0, :].rearrange("p t (n e) -> p t n e", e=2),
+                        in1=prods[:, nt * m : nt * (m + 1), 1, :].rearrange("p t (n e) -> p t n e", e=2)[:, :, :, ::-1],
                         op=ALU.add,
                     )
-                if t < len(rest):
-                    a, sq = rest[t]
-                    nc.vector.tensor_tensor(out=a[:], in0=a[:], in1=sq[:], op=ALU.add)
+            if closing:
+                nc.vector.reciprocal(out=rstd[:, 0:nt], in_=sdev[:, 0:nt])
 
-        def norm(nt, ssum, rstd):
-            sdev = work.tile([P, 4], F32, name="sdev", tag="sdev", bufs=2)
-            nc.scalar.activation(out=sdev[:, 0:nt], in_=ssum[:, 0:nt], func=ACT.Sqrt, bias=eps[:], scale=1.0 / DIM)
-            nc.vector.reciprocal(out=rstd[:, 0:nt], in_=sdev[:, 0:nt])
-
-        def finish(blk, t, half, pend, rstd):
+        def finish(blk, t, part, pend, rstd):
             r = rstd[:, t : t + 1]
             row0 = starts[blk] + P * t
-            tail = blk == len(BLOCKS) - 1
-            act_w = 512 if tail else ACT_W
-            dve_w = DIM // 2 - act_w
-            a0 = act_w * half
-            v0 = 2 * act_w + dve_w * half
-            nc.scalar.activation(out=pend[t][:, a0 : a0 + act_w], in_=pend[t][:, a0 : a0 + act_w], func=ACT.Copy, scale=r)
-            if dve_w:
-                nc.vector.tensor_scalar_mul(out=pend[t][:, v0 : v0 + dve_w], in0=pend[t][:, v0 : v0 + dve_w], scalar1=r)
-            if tail:
-                nc.sync.dma_start(out=out_rows[row0 : row0 + P, v0 : v0 + dve_w], in_=pend[t][:, v0 : v0 + dve_w])
-                nc.sync.dma_start(out=out_rows[row0 : row0 + P, a0 : a0 + act_w], in_=pend[t][:, a0 : a0 + act_w])
-            elif half == 1:
-                nc.sync.dma_start(out=out_rows[row0 : row0 + P, :], in_=pend[t][:])
+            mine = pend[:, starts[blk] % BANK // P + t, :]
+            if blk == final_blk:
+                a0 = 512 * part
+                v0 = 1024 + 1024 * part
+                nc.scalar.activation(out=mine[:, a0 : a0 + 512], in_=mine[:, a0 : a0 + 512], func=ACT.Copy, scale=r)
+                nc.vector.tensor_scalar_mul(out=mine[:, v0 : v0 + 1024], in0=mine[:, v0 : v0 + 1024], scalar1=r)
+                nc.sync.dma_start(out=out_rows[row0 : row0 + P, v0 : v0 + 1024], in_=mine[:, v0 : v0 + 1024])
+                nc.sync.dma_start(out=out_rows[row0 : row0 + P, a0 : a0 + 512], in_=mine[:, a0 : a0 + 512])
+                return
+            act_w = DIM // PARTS if blk >= ALL_ACT_FROM else ACT_W
+            a0 = act_w * part
+            nc.scalar.activation(out=mine[:, a0 : a0 + act_w], in_=mine[:, a0 : a0 + act_w], func=ACT.Copy, scale=r)
+            if part == PARTS - 1:
+                v0 = act_w * PARTS
+                if v0 < DIM:
+                    nc.vector.tensor_scalar_mul(out=mine[:, v0:DIM], in0=mine[:, v0:DIM], scalar1=r)
+                nc.sync.dma_start(out=out_rows[row0 : row0 + P, :], in_=mine)
 
         todo = []
         state = {"serial": 0, "due": 0}
@@ -276,30 +309,49 @@ def tile_causalwanselfattention_pa_kernel(tc, x_words, x_scales, w_words, w_scal
         now = 0
         for blk, n in enumerate(BLOCKS):
             nt = n // P
-            pend = [work.tile([P, DIM], F32, name="pend", tag="pend", bufs=8) for t in range(nt)]
-            acc = work.tile([P, n], F32, name="acc", tag="acc", bufs=2)
-            ssum = work.tile([P, 4], F32, name="ssum", tag="ssum", bufs=2)
-            rstd = work.tile([P, 4], F32, name="rstd", tag="rstd", bufs=3)
+            nslots = CT * n // BANK
+            if blk == final_blk:
+                sizes = LAST_GROUPS[n]
+            else:
+                sizes = (4,) * (nslots // 4) if nslots % 4 == 0 else (3,) * (nslots // 3)
+            lag = 1 if blk == final_blk else TURN_LAG
+            if starts[blk] % BANK == 0:
+                pend = work.tile([P, QUARTERS, DIM], F32, name="pend", tag="pend", bufs=2)
+            acc = work.tile([P, BANK], F32, name="acc", tag="acc", bufs=2)
+            ssum = work.tile([P, QUARTERS], F32, name="ssum", tag="ssum", bufs=3)
+            sdev = work.tile([P, QUARTERS], F32, name="sdev", tag="sdev", bufs=3)
+            rstd = work.tile([P, QUARTERS], F32, name="rstd", tag="rstd", bufs=4)
             group_u = []
-            for c in range(CT):
-                if c == 0 and 1 <= blk < len(BLOCKS) - 1:
+            done_groups = 0
+            c0 = 0
+            for s in range(nslots):
+                if s == 0 and 1 <= blk < final_blk:
                     stage_scales(blk + 1)
                     stage_codes(blk + 1)
-                    stage_freqs(blk + 1)
-                if c == GROUP and blk < len(BLOCKS) - 1:
+                if s == 0 and 1 <= blk < final_blk - 1:
+                    stage_freqs(blk + 2)
+                if s == TURN_LAG and blk < final_blk:
                     chores.extend(table_steps(blk + 1))
-                bank = project(blk, c)
-                if blk == 0 and c == 0:
+                bank = project(blk, s)
+                if blk == 0 and s == 0:
                     turn_bias_and_gain()
-                group_u.append(evacuate(bank, n, c, acc))
-                now += n
-                if c % GROUP == GROUP - 1:
-                    later(now + TURN_LAG * n, lambda blk=blk, q=c // GROUP, gu=group_u, pend=pend, acc=acc, ssum=ssum: turn(blk, q, gu, pend, acc, ssum))
+                group_u.append(evacuate(bank, blk, s, acc, blk < final_blk and s >= nslots - TURN_LAG))
+                if chores:
+                    chores[0]()
+                    chores.remove(chores[0])
+                now += 1
+                if len(group_u) == sizes[done_groups]:
+                    done_groups += 1
+                    closing = done_groups == len(sizes)
+                    carry = {}
+                    later(now + lag, lambda blk=blk, c0=c0, gu=group_u, closing=closing, acc=acc, ssum=ssum, sdev=sdev, carry=carry: turn_to_tokens(blk, c0, gu, closing, acc, ssum, sdev, carry))
+                    later(now + 2 * lag, lambda blk=blk, c0=c0, closing=closing, pend=pend, sdev=sdev, rstd=rstd, carry=carry: rotate(blk, c0, closing, pend, sdev, rstd, carry))
+                    c0 += len(group_u) * BANK // n
                     group_u = []
                 run_due(now, False)
-            later(now + NORM_LAG * n, lambda nt=nt, ssum=ssum, rstd=rstd: norm(nt, ssum, rstd))
+            norm_due = now + 2 * lag
             for t in range(nt):
-                for half in range(2):
-                    state["due"] = max(now + FINISH_LAG * n, state["due"] + FINISH_STEP)
-                    later(state["due"], lambda blk=blk, t=t, half=half, pend=pend, rstd=rstd: finish(blk, t, half, pend, rstd))
+                for part in range(2 if blk == final_blk else PARTS):
+                    state["due"] = max(norm_due + 2, state["due"] + 1)
+                    later(state["due"], lambda blk=blk, t=t, part=part, pend=pend, rstd=rstd: finish(blk, t, part, pend, rstd))
         run_due(now, True)

@@ -237,12 +237,10 @@ def tile_causalwanselfattention_pa_kernel(tc, x_words, x_scales, w_words, w_scal
                     in1=tab[:, :, t, :].unsqueeze(2).to_broadcast([P, 2, BANK // HEAD, HEAD]),
                     op=ALU.mult,
                 )
+            for a, sq in rest:
+                nc.vector.tensor_tensor(out=a[:], in0=a[:], in1=sq[:], op=ALU.add)
             if tail:
-                for a, sq in rest:
-                    nc.vector.tensor_tensor(out=a[:], in0=a[:], in1=sq[:], op=ALU.add)
-                rest = []
                 sum_of_squares()
-            carry["rest"] = rest
             carry["prods"] = prods
             carry["banks"] = len(banks)
 
@@ -250,8 +248,6 @@ def tile_causalwanselfattention_pa_kernel(tc, x_words, x_scales, w_words, w_scal
             nt = BLOCKS[blk] // P
             t0 = starts[blk] % BANK // P
             prods = carry["prods"]
-            for a, sq in carry["rest"]:
-                nc.vector.tensor_tensor(out=a[:], in0=a[:], in1=sq[:], op=ALU.add)
             chunk0 = c0 // QUARTERS
             if nt == 1:
                 k = carry["banks"]
@@ -330,7 +326,7 @@ def tile_causalwanselfattention_pa_kernel(tc, x_words, x_scales, w_words, w_scal
                     stage_codes(blk + 1)
                 if s == 0 and 1 <= blk < final_blk - 1:
                     stage_freqs(blk + 2)
-                if s == TURN_LAG and blk < final_blk:
+                if s == 4 and blk < final_blk:
                     chores.extend(table_steps(blk + 1))
                 bank = project(blk, s)
                 if blk == 0 and s == 0:

@@ -18,6 +18,7 @@ AX = mybir.AxisListType
 
 P = 128
 PASSES = DIM // 512
+HALF = PASSES // 2
 CT = DIM // P
 BANK = 512
 QUARTERS = BANK // P
@@ -48,8 +49,8 @@ def tile_causalwanselfattention_pa_kernel(tc, x_words, x_scales, w_words, w_scal
                     in_=src[:, 4 * quad : 4 * quad + 4, span].rearrange("k r n -> r k n").bitcast(I32),
                 )
 
-        def load_codes(codes, src, span):
-            nc.sync.dma_start(out=codes[:].bitcast(I32), in_=src[:, :, span].rearrange("k p n -> p k n").bitcast(I32))
+        def load_codes(codes, src, span, k0=0, k1=PASSES):
+            nc.sync.dma_start(out=codes[:, k0:k1, :].bitcast(I32), in_=src[k0:k1, :, span].rearrange("k p n -> p k n").bitcast(I32))
 
         starts = [sum(BLOCKS[:i]) for i in range(len(BLOCKS))]
         staged = {}
@@ -62,11 +63,12 @@ def tile_causalwanselfattention_pa_kernel(tc, x_words, x_scales, w_words, w_scal
             load_scales(xs, x_scales, slice(starts[blk], starts[blk] + n))
             staged[blk]["xs"] = xs
 
-        def stage_codes(blk):
+        def stage_codes(blk, k0=0, k1=PASSES):
             n = BLOCKS[blk]
-            xc = work.tile([P, PASSES, 2 * n], U8, name="xc", tag="xc", bufs=2, align_bytes=64)
-            load_codes(xc, x_words, slice(2 * starts[blk], 2 * (starts[blk] + n)))
-            staged[blk]["xc"] = xc
+            if k0 == 0:
+                xc = work.tile([P, PASSES, 2 * n], U8, name="xc", tag="xc", bufs=2, align_bytes=64)
+                staged[blk]["xc"] = xc
+            load_codes(staged[blk]["xc"], x_words, slice(2 * starts[blk], 2 * (starts[blk] + n)), k0, k1)
 
         def stage_freqs(blk):
             n = BLOCKS[blk]
@@ -100,8 +102,8 @@ def tile_causalwanselfattention_pa_kernel(tc, x_words, x_scales, w_words, w_scal
         def load_w_scales(q):
             load_scales(ws[q], w_scales, slice(BANK * q, BANK * (q + 1)))
 
-        def load_w_codes(q):
-            load_codes(wc[q], w_words, slice(2 * BANK * q, 2 * BANK * (q + 1)))
+        def load_w_codes(q, k0=0, k1=PASSES):
+            load_codes(wc[q], w_words, slice(2 * BANK * q, 2 * BANK * (q + 1)), k0, k1)
 
         eps = keep.tile([P, 1], F32, name="eps")
         nc.gpsimd.memset(eps[:], EPS)
@@ -115,10 +117,12 @@ def tile_causalwanselfattention_pa_kernel(tc, x_words, x_scales, w_words, w_scal
         stage_freqs(0)
         stage_freqs(1)
         stage_freqs(2)
-        stage_codes(0)
-        load_w_codes(0)
+        stage_codes(0, 0, HALF)
+        load_w_codes(0, 0, HALF)
         load_w_scales(0)
         stage_scales(0)
+        stage_codes(0, HALF, PASSES)
+        load_w_codes(0, HALF, PASSES)
         nc.scalar.dma_start(out=bg_rows[0:CT, :], in_=b.rearrange("(c p) -> c p", p=P))
         nc.scalar.dma_start(out=bg_rows[32 : 32 + CT, :], in_=g.rearrange("(c p) -> c p", p=P))
         load_w_scales(1)
@@ -151,14 +155,13 @@ def tile_causalwanselfattention_pa_kernel(tc, x_words, x_scales, w_words, w_scal
         owed = []
         chores = []
 
-        def project(blk, s):
+        def project(blk, s, bank, k0, k1):
             n = BLOCKS[blk]
             xc = staged[blk]["xc"]
             xs = staged[blk]["xs"]
-            bank = psum.tile([P, BANK], F32, name="mx", tag="mx")
             for j in range(BANK // n):
                 q, i = divmod(s * (BANK // n) + j, QUARTERS)
-                for k in range(PASSES):
+                for k in range(k0, k1):
                     nc.tensor.matmul_mx(
                         out=bank[:, n * j : n * (j + 1)],
                         lhsT=wc[q][:, k, 2 * P * i : 2 * P * (i + 1)].bitcast(FP4X4),
@@ -168,7 +171,6 @@ def tile_causalwanselfattention_pa_kernel(tc, x_words, x_scales, w_words, w_scal
                         start=(k == 0),
                         stop=(k == PASSES - 1),
                     )
-            return bank
 
         def evacuate(bank, blk, s, acc, at_once):
             n = BLOCKS[blk]
@@ -303,6 +305,7 @@ def tile_causalwanselfattention_pa_kernel(tc, x_words, x_scales, w_words, w_scal
                 todo.remove(e)
 
         now = 0
+        first_banks = []
         for blk, n in enumerate(BLOCKS):
             nt = n // P
             nslots = CT * n // BANK
@@ -328,7 +331,17 @@ def tile_causalwanselfattention_pa_kernel(tc, x_words, x_scales, w_words, w_scal
                     stage_freqs(blk + 2)
                 if s == 4 and blk < final_blk:
                     chores.extend(table_steps(blk + 1))
-                bank = project(blk, s)
+                if blk == 0 and s == 0:
+                    for s2 in range(QUARTERS):
+                        early = psum.tile([P, BANK], F32, name="mx", tag="mx")
+                        first_banks.append(early)
+                        project(0, s2, early, 0, HALF)
+                if blk == 0 and s < QUARTERS:
+                    bank = first_banks[s]
+                    project(0, s, bank, HALF, PASSES)
+                else:
+                    bank = psum.tile([P, BANK], F32, name="mx", tag="mx")
+                    project(blk, s, bank, 0, PASSES)
                 if blk == 0 and s == 0:
                     turn_bias_and_gain()
                 group_u.append(evacuate(bank, blk, s, acc, blk < final_blk and s >= nslots - TURN_LAG))

@@ -28,6 +28,8 @@ TURN_LAG = 2
 ACT_W = 1024
 PARTS = 2
 ALL_ACT_FROM = 4
+LAST_PIECES = ((0, 768), (768, 1536), (1536, 2560), (2560, 3072))
+LAST_SCALED_FROM = 2560
 
 
 def tile_causalwanselfattention_pa_kernel(tc, x_words, x_scales, w_words, w_scales, b, g, freqs, out):
@@ -112,7 +114,7 @@ def tile_causalwanselfattention_pa_kernel(tc, x_words, x_scales, w_words, w_scal
         ident = keep.tile([P, P], F32, name="ident")
         make_identity(nc, ident[:])
         warm = keep.tile([P, 1], F32, name="warm")
-        nc.scalar.activation(out=warm[:], in_=eps[:], func=ACT.Sqrt)
+        nc.scalar.activation(out=warm[:], in_=eps[:], func=ACT.Abs_reciprocal_sqrt)
 
         stage_freqs(0)
         stage_freqs(1)
@@ -178,26 +180,43 @@ def tile_causalwanselfattention_pa_kernel(tc, x_words, x_scales, w_words, w_scal
             sq = acc
             if s > 0:
                 sq = work.tile([P, BANK], F32, name="sq", tag="sq", bufs=6)
-            for j in range(BANK // n):
-                c = s * (BANK // n) + j
-                span = slice(n * j, n * (j + 1))
-                nc.scalar.activation(out=u[:, span], in_=bank[:, span], func=ACT.Identity, bias=bgcol[:, c : c + 1], scale=cols[:, 32 + c : 33 + c])
-            for j in range(BANK // n):
-                c = s * (BANK // n) + j
-                span = slice(n * j, n * (j + 1))
-                nc.scalar.activation(out=sq[:, span], in_=bank[:, span], func=ACT.Square, bias=cols[:, c : c + 1], scale=1.0)
+            last_of_all = blk == final_blk and s == CT * n // BANK - 1
+            for what in ("sq", "u") if last_of_all else ("u", "sq"):
+                for j in range(BANK // n):
+                    c = s * (BANK // n) + j
+                    span = slice(n * j, n * (j + 1))
+                    if what == "u":
+                        nc.scalar.activation(out=u[:, span], in_=bank[:, span], func=ACT.Identity, bias=bgcol[:, c : c + 1], scale=cols[:, 32 + c : 33 + c])
+                    else:
+                        nc.scalar.activation(out=sq[:, span], in_=bank[:, span], func=ACT.Square, bias=cols[:, c : c + 1], scale=1.0)
             if s > 0 and at_once:
                 nc.vector.tensor_tensor(out=acc[:], in0=acc[:], in1=sq[:], op=ALU.add)
             elif s > 0:
                 owed.append((acc, sq))
             return u
 
-        def turn_to_tokens(blk, c0, group_u, closing, acc, ssum, sdev, carry):
+        def sum_of_squares(blk, sources, ssum, rstd):
+            n = BLOCKS[blk]
+            nt = n // P
+            sums = psum.tile([P, BANK], F32, name="mx", tag="mx")
+            junk = work.tile([P, BANK], F32, name="junk", tag="junk", bufs=1)
+            for t in range(nt):
+                parts = [src[:, n * j + P * t : n * j + P * (t + 1)] for src in sources for j in range(BANK // n)]
+                for i in range(len(parts)):
+                    nc.tensor.matmul(out=sums[:, P * t : P * (t + 1)], lhsT=parts[i], rhs=ident[:], is_transpose=True, start=(i == 0), stop=(i == len(parts) - 1))
+            for t in range(nt):
+                nc.scalar.activation(out=junk[:, P * t : P * (t + 1)], in_=sums[:, P * t : P * (t + 1)], func=ACT.Copy, accum_out=ssum[:, t : t + 1])
+            nc.scalar.activation(out=rstd[:, 0:nt], in_=ssum[:, 0:nt], func=ACT.Abs_reciprocal_sqrt, bias=eps[:], scale=1.0 / DIM)
+
+        def turn_to_tokens(blk, c0, group_u, closing, acc, ssum, rstd, carry):
             n = BLOCKS[blk]
             nt = n // P
             per_slot = BANK // n
             tab = staged[blk]["tab"]
             tail = closing and blk == final_blk
+            if tail:
+                sum_of_squares(blk, [acc] + [sq for a, sq in owed], ssum, rstd)
+                owed.clear()
             banks = []
             for m in range(len(group_u) * per_slot // QUARTERS):
                 for t in range(nt):
@@ -207,46 +226,45 @@ def tile_causalwanselfattention_pa_kernel(tc, x_words, x_scales, w_words, w_scal
                         nc.tensor.transpose(out=bank[:, P * i : P * (i + 1)], in_=group_u[si][:, n * j + P * t : n * j + P * (t + 1)], identity=ident[:])
                     banks.append((bank, t))
 
-            def sum_of_squares():
-                sums = psum.tile([P, BANK], F32, name="mx", tag="mx")
-                for i in range(QUARTERS):
-                    nc.tensor.transpose(out=sums[:, P * i : P * (i + 1)], in_=acc[:, P * i : P * (i + 1)], identity=ident[:])
-                junk = work.tile([P, BANK], F32, name="junk", tag="junk", bufs=1)
-                by_token = sums[:].rearrange("p (j t k) -> p t j k", t=nt, k=P)
-                for t in range(nt):
-                    nc.scalar.activation(
-                        out=junk[:, per_slot * P * t : per_slot * P * (t + 1)].rearrange("p (j k) -> p j k", k=P),
-                        in_=by_token[:, t, :, :], func=ACT.Copy, accum_out=ssum[:, t : t + 1],
-                    )
-                nc.scalar.activation(out=sdev[:, 0:nt], in_=ssum[:, 0:nt], func=ACT.Sqrt, bias=eps[:], scale=1.0 / DIM)
-
             if closing and not tail:
-                sum_of_squares()
+                sum_of_squares(blk, [acc], ssum, rstd)
             mine = list(owed)
             owed.clear()
-            room = 0 if tail else len(banks) - 1
+            room = len(banks) - 1 if blk < final_blk or c0 == 0 else 0
             if mine and room:
                 nc.vector.tensor_copy(out=flag[:], in_=mine[0][0][:, 0:1])
             for a, sq in mine[:room]:
                 nc.gpsimd.tensor_tensor(out=a[:], in0=a[:], in1=sq[:], op=ALU.add)
             rest = mine[room:]
+            if blk == final_blk:
+                owed.extend(rest)
+                rest = []
             prods = work.tile([P, QUARTERS, 2, BANK], F32, name="prods", tag="prods", bufs=1)
             for i in range(len(banks)):
                 bank, t = banks[i]
-                nc.vector.tensor_tensor(
-                    out=prods[:, i, :, :].rearrange("p a (h d) -> p a h d", d=HEAD),
-                    in0=bank[:].unsqueeze(1).to_broadcast([P, 2, BANK]).rearrange("p a (h d) -> p a h d", d=HEAD),
-                    in1=tab[:, :, t, :].unsqueeze(2).to_broadcast([P, 2, BANK // HEAD, HEAD]),
-                    op=ALU.mult,
-                )
+                if tail:
+                    for a in range(2):
+                        nc.vector.scalar_tensor_tensor(
+                            out=prods[:, i, a, :].rearrange("p (h d) -> p h d", d=HEAD),
+                            in0=bank[:].rearrange("p (h d) -> p h d", d=HEAD),
+                            scalar=rstd[:, t : t + 1],
+                            in1=tab[:, a, t, :].unsqueeze(1).to_broadcast([P, BANK // HEAD, HEAD]),
+                            op0=ALU.mult,
+                            op1=ALU.mult,
+                        )
+                else:
+                    nc.vector.tensor_tensor(
+                        out=prods[:, i, :, :].rearrange("p a (h d) -> p a h d", d=HEAD),
+                        in0=bank[:].unsqueeze(1).to_broadcast([P, 2, BANK]).rearrange("p a (h d) -> p a h d", d=HEAD),
+                        in1=tab[:, :, t, :].unsqueeze(2).to_broadcast([P, 2, BANK // HEAD, HEAD]),
+                        op=ALU.mult,
+                    )
             for a, sq in rest:
                 nc.vector.tensor_tensor(out=a[:], in0=a[:], in1=sq[:], op=ALU.add)
-            if tail:
-                sum_of_squares()
             carry["prods"] = prods
             carry["banks"] = len(banks)
 
-        def rotate(blk, c0, closing, pend, sdev, rstd, carry):
+        def rotate(blk, c0, pend, carry):
             nt = BLOCKS[blk] // P
             t0 = starts[blk] % BANK // P
             prods = carry["prods"]
@@ -267,20 +285,16 @@ def tile_causalwanselfattention_pa_kernel(tc, x_words, x_scales, w_words, w_scal
                         in1=prods[:, nt * m : nt * (m + 1), 1, :].rearrange("p t (n e) -> p t n e", e=2)[:, :, :, ::-1],
                         op=ALU.add,
                     )
-            if closing:
-                nc.vector.reciprocal(out=rstd[:, 0:nt], in_=sdev[:, 0:nt])
 
         def finish(blk, t, part, pend, rstd):
             r = rstd[:, t : t + 1]
             row0 = starts[blk] + P * t
             mine = pend[:, starts[blk] % BANK // P + t, :]
             if blk == final_blk:
-                a0 = 512 * part
-                v0 = 1024 + 1024 * part
-                nc.scalar.activation(out=mine[:, a0 : a0 + 512], in_=mine[:, a0 : a0 + 512], func=ACT.Copy, scale=r)
-                nc.vector.tensor_scalar_mul(out=mine[:, v0 : v0 + 1024], in0=mine[:, v0 : v0 + 1024], scalar1=r)
-                nc.sync.dma_start(out=out_rows[row0 : row0 + P, v0 : v0 + 1024], in_=mine[:, v0 : v0 + 1024])
-                nc.sync.dma_start(out=out_rows[row0 : row0 + P, a0 : a0 + 512], in_=mine[:, a0 : a0 + 512])
+                a0, a1 = LAST_PIECES[part]
+                if a1 <= LAST_SCALED_FROM:
+                    nc.scalar.activation(out=mine[:, a0:a1], in_=mine[:, a0:a1], func=ACT.Copy, scale=r)
+                nc.sync.dma_start(out=out_rows[row0 : row0 + P, a0:a1], in_=mine[:, a0:a1])
                 return
             act_w = DIM // PARTS if blk >= ALL_ACT_FROM else ACT_W
             a0 = act_w * part
@@ -318,7 +332,6 @@ def tile_causalwanselfattention_pa_kernel(tc, x_words, x_scales, w_words, w_scal
                 pend = work.tile([P, QUARTERS, DIM], F32, name="pend", tag="pend", bufs=2)
             acc = work.tile([P, BANK], F32, name="acc", tag="acc", bufs=2)
             ssum = work.tile([P, QUARTERS], F32, name="ssum", tag="ssum", bufs=3)
-            sdev = work.tile([P, QUARTERS], F32, name="sdev", tag="sdev", bufs=3)
             rstd = work.tile([P, QUARTERS], F32, name="rstd", tag="rstd", bufs=4)
             group_u = []
             done_groups = 0
@@ -353,14 +366,14 @@ def tile_causalwanselfattention_pa_kernel(tc, x_words, x_scales, w_words, w_scal
                     done_groups += 1
                     closing = done_groups == len(sizes)
                     carry = {}
-                    later(now + lag, lambda blk=blk, c0=c0, gu=group_u, closing=closing, acc=acc, ssum=ssum, sdev=sdev, carry=carry: turn_to_tokens(blk, c0, gu, closing, acc, ssum, sdev, carry))
-                    later(now + 2 * lag, lambda blk=blk, c0=c0, closing=closing, pend=pend, sdev=sdev, rstd=rstd, carry=carry: rotate(blk, c0, closing, pend, sdev, rstd, carry))
+                    later(now + lag, lambda blk=blk, c0=c0, gu=group_u, closing=closing, acc=acc, ssum=ssum, rstd=rstd, carry=carry: turn_to_tokens(blk, c0, gu, closing, acc, ssum, rstd, carry))
+                    later(now + 2 * lag, lambda blk=blk, c0=c0, pend=pend, carry=carry: rotate(blk, c0, pend, carry))
                     c0 += len(group_u) * BANK // n
                     group_u = []
                 run_due(now, False)
             norm_due = now + 2 * lag
             for t in range(nt):
-                for part in range(2 if blk == final_blk else PARTS):
+                for part in range(len(LAST_PIECES) if blk == final_blk else PARTS):
                     state["due"] = max(norm_due + 2, state["due"] + 1)
                     later(state["due"], lambda blk=blk, t=t, part=part, pend=pend, rstd=rstd: finish(blk, t, part, pend, rstd))
         run_due(now, True)

@@ -22,14 +22,15 @@ HALF = PASSES // 2
 CT = DIM // P
 BANK = 512
 QUARTERS = BANK // P
-BLOCKS = (512, 512, 512, 256, 128, 128)
+BLOCKS = (512, 512, 512, 256, 256)
 LAST_GROUPS = {128: (3, 2, 1), 256: (4, 4, 2, 2), 512: (4, 4, 4, 4, 4, 4)}
 TURN_LAG = 2
 ACT_W = 1024
 PARTS = 2
 ALL_ACT_FROM = 4
-LAST_PIECES = ((0, 768), (768, 1536), (1536, 2560), (2560, 3072))
+LAST_PIECES = ((0, 1024), (1024, 2048), (2048, 2560), (2560, 3072))
 LAST_SCALED_FROM = 2560
+LAST_ADDS_BEFORE = 16
 
 
 def tile_causalwanselfattention_pa_kernel(tc, x_words, x_scales, w_words, w_scales, b, g, freqs, out):
@@ -43,8 +44,9 @@ def tile_causalwanselfattention_pa_kernel(tc, x_words, x_scales, w_words, w_scal
         psum = ctx.enter_context(tc.psum_pool(name="psum", bufs=4))
         ctx.enter_context(tc.manual_schedule())
 
-        def load_scales(plane, src, span):
-            nc.vector.memset(plane[:].bitcast(I32), 0)
+        def load_scales(plane, src, span, fresh=True):
+            if fresh:
+                nc.vector.memset(plane[:].bitcast(I32), 0)
             for quad in range(4):
                 nc.sync.dma_start(
                     out=plane[32 * quad : 32 * quad + 4, :, :].bitcast(I32),
@@ -62,7 +64,7 @@ def tile_causalwanselfattention_pa_kernel(tc, x_words, x_scales, w_words, w_scal
         def stage_scales(blk):
             n = BLOCKS[blk]
             xs = work.tile([P, PASSES, n], U8, name="xs", tag="xs", bufs=2, align_bytes=64)
-            load_scales(xs, x_scales, slice(starts[blk], starts[blk] + n))
+            load_scales(xs, x_scales, slice(starts[blk], starts[blk] + n), blk < 2)
             staged[blk]["xs"] = xs
 
         def stage_codes(blk, k0=0, k1=PASSES):
@@ -72,20 +74,20 @@ def tile_causalwanselfattention_pa_kernel(tc, x_words, x_scales, w_words, w_scal
                 staged[blk]["xc"] = xc
             load_codes(staged[blk]["xc"], x_words, slice(2 * starts[blk], 2 * (starts[blk] + n)), k0, k1)
 
-        def stage_freqs(blk):
-            n = BLOCKS[blk]
-            fr = work.tile([P, n // P, HEAD], BF16, name="fr", tag="fr", bufs=3)
-            nc.gpsimd.dma_start(out=fr[:], in_=freqs[starts[blk] : starts[blk] + n, :].rearrange("(t p) d -> p t d", p=P))
-            staged[blk]["fr"] = fr
+        tables = {}
 
-        def table_steps(blk):
-            nt = BLOCKS[blk] // P
-            pairs = nt * HEAD // 2
-            fr = staged[blk]["fr"][:].rearrange("p t (j e) -> p (t j) e", e=2)
-            tab = work.tile([P, 2, nt, HEAD], BF16, name="tab", tag="tab", bufs=2)
+        def stage_freqs(sb):
+            fr = work.tile([P, QUARTERS, HEAD], BF16, name="fr", tag="fr", bufs=3)
+            nc.gpsimd.dma_start(out=fr[:], in_=freqs[BANK * sb : BANK * (sb + 1), :].rearrange("(t p) d -> p t d", p=P))
+            tables[sb] = {"fr": fr}
+
+        def table_steps(sb):
+            pairs = QUARTERS * HEAD // 2
+            fr = tables[sb]["fr"][:].rearrange("p t (j e) -> p (t j) e", e=2)
+            tab = work.tile([P, 2, QUARTERS, HEAD], BF16, name="tab", tag="tab", bufs=2)
             ccv = tab[:, 0, :, :].rearrange("p t (j e) -> p (t j) e", e=2)
             snv = tab[:, 1, :, :].rearrange("p t (j e) -> p (t j) e", e=2)
-            staged[blk]["tab"] = tab
+            tables[sb]["tab"] = tab
 
             return [
                 lambda: nc.scalar.activation(out=ccv, in_=fr[:, :, 0:1].to_broadcast([P, pairs, 2]), func=ACT.Copy),
@@ -198,21 +200,35 @@ def tile_causalwanselfattention_pa_kernel(tc, x_words, x_scales, w_words, w_scal
         def sum_of_squares(blk, sources, ssum, rstd):
             n = BLOCKS[blk]
             nt = n // P
-            sums = psum.tile([P, BANK], F32, name="mx", tag="mx")
             junk = work.tile([P, BANK], F32, name="junk", tag="junk", bufs=1)
+            sums = []
+            if len(sources) == 1:
+                bank = psum.tile([P, BANK], F32, name="mx", tag="mx")
+                for t in range(nt):
+                    sums.append(bank[:, P * t : P * (t + 1)])
+            else:
+                for t in range(nt):
+                    bank = psum.tile([P, BANK], F32, name="mx", tag="mx")
+                    sums.append(bank[:, 0:P])
+            per_slot = BANK // n
+            if len(sources) == 1:
+                order = [(0, t, j) for t in range(nt) for j in range(per_slot)]
+            else:
+                order = [(i, t, j) for i in range(len(sources)) for t in range(nt) for j in range(per_slot)]
+            for i, t, j in order:
+                nc.tensor.matmul(
+                    out=sums[t], lhsT=sources[i][:, n * j + P * t : n * j + P * (t + 1)], rhs=ident[:], is_transpose=True,
+                    start=(i == 0 and j == 0), stop=(i == len(sources) - 1 and j == per_slot - 1),
+                )
             for t in range(nt):
-                parts = [src[:, n * j + P * t : n * j + P * (t + 1)] for src in sources for j in range(BANK // n)]
-                for i in range(len(parts)):
-                    nc.tensor.matmul(out=sums[:, P * t : P * (t + 1)], lhsT=parts[i], rhs=ident[:], is_transpose=True, start=(i == 0), stop=(i == len(parts) - 1))
-            for t in range(nt):
-                nc.scalar.activation(out=junk[:, P * t : P * (t + 1)], in_=sums[:, P * t : P * (t + 1)], func=ACT.Copy, accum_out=ssum[:, t : t + 1])
+                nc.scalar.activation(out=junk[:, P * t : P * (t + 1)], in_=sums[t], func=ACT.Copy, accum_out=ssum[:, t : t + 1])
             nc.scalar.activation(out=rstd[:, 0:nt], in_=ssum[:, 0:nt], func=ACT.Abs_reciprocal_sqrt, bias=eps[:], scale=1.0 / DIM)
 
         def turn_to_tokens(blk, c0, group_u, closing, acc, ssum, rstd, carry):
             n = BLOCKS[blk]
             nt = n // P
             per_slot = BANK // n
-            tab = staged[blk]["tab"]
+            tab = tables[starts[blk] // BANK]["tab"][:, :, starts[blk] % BANK // P : (starts[blk] % BANK + n) // P, :]
             tail = closing and blk == final_blk
             if tail:
                 sum_of_squares(blk, [acc] + [sq for a, sq in owed], ssum, rstd)
@@ -230,7 +246,7 @@ def tile_causalwanselfattention_pa_kernel(tc, x_words, x_scales, w_words, w_scal
                 sum_of_squares(blk, [acc], ssum, rstd)
             mine = list(owed)
             owed.clear()
-            room = len(banks) - 1 if blk < final_blk or c0 == 0 else 0
+            room = len(banks) - 1 if blk < final_blk or c0 < LAST_ADDS_BEFORE else 0
             if mine and room:
                 nc.vector.tensor_copy(out=flag[:], in_=mine[0][0][:, 0:1])
             for a, sq in mine[:room]:
@@ -277,6 +293,15 @@ def tile_causalwanselfattention_pa_kernel(tc, x_words, x_scales, w_words, w_scal
                     in1=prods[:, 0:k, 1, :].rearrange("p m (n e) -> p m n e", e=2)[:, :, :, ::-1],
                     op=ALU.add,
                 )
+            elif nt == 2:
+                k = carry["banks"] // nt
+                for t in range(nt):
+                    nc.vector.tensor_tensor(
+                        out=pend[:, t0 + t, BANK * chunk0 : BANK * (chunk0 + k)].rearrange("p (m n e) -> p m n e", m=k, e=2),
+                        in0=prods[:, t : nt * k : nt, 0, :].rearrange("p m (n e) -> p m n e", e=2),
+                        in1=prods[:, t : nt * k : nt, 1, :].rearrange("p m (n e) -> p m n e", e=2)[:, :, :, ::-1],
+                        op=ALU.add,
+                    )
             else:
                 for m in range(carry["banks"] // nt):
                     nc.vector.tensor_tensor(
@@ -340,10 +365,11 @@ def tile_causalwanselfattention_pa_kernel(tc, x_words, x_scales, w_words, w_scal
                 if s == 0 and 1 <= blk < final_blk:
                     stage_scales(blk + 1)
                     stage_codes(blk + 1)
-                if s == 0 and 1 <= blk < final_blk - 1:
-                    stage_freqs(blk + 2)
-                if s == 4 and blk < final_blk:
-                    chores.extend(table_steps(blk + 1))
+                sb = starts[blk] // BANK
+                if s == 0 and starts[blk] % BANK == 0 and 1 <= sb < ROWS // BANK - 2:
+                    stage_freqs(sb + 2)
+                if s == 4 and starts[blk] % BANK == 0 and sb < ROWS // BANK - 1:
+                    chores.extend(table_steps(sb + 1))
                 if blk == 0 and s == 0:
                     for s2 in range(QUARTERS):
                         early = psum.tile([P, BANK], F32, name="mx", tag="mx")
@@ -372,8 +398,10 @@ def tile_causalwanselfattention_pa_kernel(tc, x_words, x_scales, w_words, w_scal
                     group_u = []
                 run_due(now, False)
             norm_due = now + 2 * lag
-            for t in range(nt):
-                for part in range(len(LAST_PIECES) if blk == final_blk else PARTS):
-                    state["due"] = max(norm_due + 2, state["due"] + 1)
-                    later(state["due"], lambda blk=blk, t=t, part=part, pend=pend, rstd=rstd: finish(blk, t, part, pend, rstd))
+            steps = [(t, part) for t in range(nt) for part in range(PARTS)]
+            if blk == final_blk:
+                steps = [(t, part) for part in range(len(LAST_PIECES)) for t in range(nt)]
+            for t, part in steps:
+                state["due"] = max(norm_due + 2, state["due"] + 1)
+                later(state["due"], lambda blk=blk, t=t, part=part, pend=pend, rstd=rstd: finish(blk, t, part, pend, rstd))
         run_due(now, True)

@@ -18,7 +18,7 @@ AX = mybir.AxisListType
 
 P = 128
 PASSES = DIM // 512
-HALF = PASSES // 2
+HALF = 2
 CT = DIM // P
 BANK = 512
 QUARTERS = BANK // P
@@ -63,14 +63,14 @@ def tile_causalwanselfattention_pa_kernel(tc, x_words, x_scales, w_words, w_scal
 
         def stage_scales(blk):
             n = BLOCKS[blk]
-            xs = work.tile([P, PASSES, n], U8, name="xs", tag="xs", bufs=2, align_bytes=64)
+            xs = work.tile([P, PASSES, n], U8, name="xs", tag="xs", bufs=2, align_bytes=256)
             load_scales(xs, x_scales, slice(starts[blk], starts[blk] + n), blk < 2)
             staged[blk]["xs"] = xs
 
         def stage_codes(blk, k0=0, k1=PASSES):
             n = BLOCKS[blk]
             if k0 == 0:
-                xc = work.tile([P, PASSES, 2 * n], U8, name="xc", tag="xc", bufs=2, align_bytes=64)
+                xc = work.tile([P, PASSES, 2 * n], U8, name="xc", tag="xc", bufs=2, align_bytes=256)
                 staged[blk]["xc"] = xc
             load_codes(staged[blk]["xc"], x_words, slice(2 * starts[blk], 2 * (starts[blk] + n)), k0, k1)
 
@@ -98,8 +98,8 @@ def tile_causalwanselfattention_pa_kernel(tc, x_words, x_scales, w_words, w_scal
         wc = []
         ws = []
         for q in range(CT // QUARTERS):
-            wcq = keep.tile([P, PASSES, 2 * BANK], U8, name="wc%d" % q, align_bytes=64)
-            wsq = keep.tile([P, PASSES, BANK], U8, name="ws%d" % q, align_bytes=64)
+            wcq = keep.tile([P, PASSES, 2 * BANK], U8, name="wc%d" % q, align_bytes=256)
+            wsq = keep.tile([P, PASSES, BANK], U8, name="ws%d" % q, align_bytes=256)
             wc.append(wcq)
             ws.append(wsq)
 

@@ -28,6 +28,8 @@ TURN_LAG = 2
 ACT_W = 1024
 PARTS = 2
 ALL_ACT_FROM = 4
+FIN = 4
+LANES = 2
 LAST_PIECES = ((0, 1024), (1024, 2048), (2048, 2560), (2560, 3072))
 LAST_SCALED_FROM = 2560
 LAST_ADDS_BEFORE = 16
@@ -157,6 +159,7 @@ def tile_causalwanselfattention_pa_kernel(tc, x_words, x_scales, w_words, w_scal
             nc.vector.tensor_tensor(out=bgcol[:], in0=cols[:, 0:CT], in1=cols[:, 32 : 32 + CT], op=ALU.mult)
 
         owed = []
+        complete = []
         chores = []
 
         def project(blk, s, bank, k0, k1):
@@ -176,12 +179,9 @@ def tile_causalwanselfattention_pa_kernel(tc, x_words, x_scales, w_words, w_scal
                         stop=(k == PASSES - 1),
                     )
 
-        def evacuate(bank, blk, s, acc, at_once):
+        def evacuate(bank, blk, s, sq):
             n = BLOCKS[blk]
             u = work.tile([P, BANK], F32, name="u", tag="u", bufs=8)
-            sq = acc
-            if s > 0:
-                sq = work.tile([P, BANK], F32, name="sq", tag="sq", bufs=6)
             last_of_all = blk == final_blk and s == CT * n // BANK - 1
             for what in ("sq", "u") if last_of_all else ("u", "sq"):
                 for j in range(BANK // n):
@@ -191,16 +191,12 @@ def tile_causalwanselfattention_pa_kernel(tc, x_words, x_scales, w_words, w_scal
                         nc.scalar.activation(out=u[:, span], in_=bank[:, span], func=ACT.Identity, bias=bgcol[:, c : c + 1], scale=cols[:, 32 + c : 33 + c])
                     else:
                         nc.scalar.activation(out=sq[:, span], in_=bank[:, span], func=ACT.Square, bias=cols[:, c : c + 1], scale=1.0)
-            if s > 0 and at_once:
-                nc.vector.tensor_tensor(out=acc[:], in0=acc[:], in1=sq[:], op=ALU.add)
-            elif s > 0:
-                owed.append((acc, sq))
             return u
 
         def sum_of_squares(blk, sources, ssum, rstd):
             n = BLOCKS[blk]
             nt = n // P
-            junk = work.tile([P, BANK], F32, name="junk", tag="junk", bufs=1)
+            junk = work.tile([P, P], BF16, name="junk", tag="junk", bufs=1)
             sums = []
             if len(sources) == 1:
                 bank = psum.tile([P, BANK], F32, name="mx", tag="mx")
@@ -221,7 +217,7 @@ def tile_causalwanselfattention_pa_kernel(tc, x_words, x_scales, w_words, w_scal
                     start=(i == 0 and j == 0), stop=(i == len(sources) - 1 and j == per_slot - 1),
                 )
             for t in range(nt):
-                nc.scalar.activation(out=junk[:, P * t : P * (t + 1)], in_=sums[t], func=ACT.Copy, accum_out=ssum[:, t : t + 1])
+                nc.scalar.activation(out=junk[:], in_=sums[t], func=ACT.Copy, accum_out=ssum[:, t : t + 1])
             nc.scalar.activation(out=rstd[:, 0:nt], in_=ssum[:, 0:nt], func=ACT.Abs_reciprocal_sqrt, bias=eps[:], scale=1.0 / DIM)
 
         def turn_to_tokens(blk, c0, group_u, closing, acc, ssum, rstd, carry):
@@ -231,7 +227,7 @@ def tile_causalwanselfattention_pa_kernel(tc, x_words, x_scales, w_words, w_scal
             tab = tables[starts[blk] // BANK]["tab"][:, :, starts[blk] % BANK // P : (starts[blk] % BANK + n) // P, :]
             tail = closing and blk == final_blk
             if tail:
-                sum_of_squares(blk, [acc] + [sq for a, sq in owed], ssum, rstd)
+                sum_of_squares(blk, [x[:, i, :] for x in [acc] + [sq for a, sq in owed] for i in range(LANES)], ssum, rstd)
                 owed.clear()
             banks = []
             for m in range(len(group_u) * per_slot // QUARTERS):
@@ -242,19 +238,20 @@ def tile_causalwanselfattention_pa_kernel(tc, x_words, x_scales, w_words, w_scal
                         nc.tensor.transpose(out=bank[:, P * i : P * (i + 1)], in_=group_u[si][:, n * j + P * t : n * j + P * (t + 1)], identity=ident[:])
                     banks.append((bank, t))
 
-            if closing and not tail:
-                sum_of_squares(blk, [acc], ssum, rstd)
-            mine = list(owed)
-            owed.clear()
-            room = len(banks) - 1 if blk < final_blk or c0 < LAST_ADDS_BEFORE else 0
-            if mine and room:
-                nc.vector.tensor_copy(out=flag[:], in_=mine[0][0][:, 0:1])
-            for a, sq in mine[:room]:
+            for b2, a2, ss2, rs2 in complete:
+                sum_of_squares(b2, [a2[:, 0, :]], ss2, rs2)
+            complete.clear()
+            room = len(banks) // LANES if blk < final_blk or c0 < LAST_ADDS_BEFORE else 0
+            mine = owed[:room]
+            for job in mine:
+                owed.remove(job)
+            if mine:
+                nc.vector.tensor_copy(out=flag[:], in_=mine[0][0][:, 0, 0:1])
+            for a, sq in mine:
                 nc.gpsimd.tensor_tensor(out=a[:], in0=a[:], in1=sq[:], op=ALU.add)
-            rest = mine[room:]
-            if blk == final_blk:
-                owed.extend(rest)
-                rest = []
+            if closing and not tail:
+                nc.gpsimd.tensor_tensor(out=acc[:, 0, :], in0=acc[:, 0, :], in1=acc[:, 1, :], op=ALU.add)
+                complete.append((blk, acc, ssum, rstd))
             prods = work.tile([P, QUARTERS, 2, BANK], F32, name="prods", tag="prods", bufs=1)
             for i in range(len(banks)):
                 bank, t = banks[i]
@@ -275,8 +272,6 @@ def tile_causalwanselfattention_pa_kernel(tc, x_words, x_scales, w_words, w_scal
                         in1=tab[:, :, t, :].unsqueeze(2).to_broadcast([P, 2, BANK // HEAD, HEAD]),
                         op=ALU.mult,
                     )
-            for a, sq in rest:
-                nc.vector.tensor_tensor(out=a[:], in0=a[:], in1=sq[:], op=ALU.add)
             carry["prods"] = prods
             carry["banks"] = len(banks)
 
@@ -355,7 +350,8 @@ def tile_causalwanselfattention_pa_kernel(tc, x_words, x_scales, w_words, w_scal
             lag = 1 if blk == final_blk else TURN_LAG
             if starts[blk] % BANK == 0:
                 pend = work.tile([P, QUARTERS, DIM], F32, name="pend", tag="pend", bufs=2)
-            acc = work.tile([P, BANK], F32, name="acc", tag="acc", bufs=2)
+            acc = work.tile([P, LANES, BANK], F32, name="acc", tag="acc", bufs=2)
+            sq = acc
             ssum = work.tile([P, QUARTERS], F32, name="ssum", tag="ssum", bufs=3)
             rstd = work.tile([P, QUARTERS], F32, name="rstd", tag="rstd", bufs=4)
             group_u = []
@@ -383,7 +379,11 @@ def tile_causalwanselfattention_pa_kernel(tc, x_words, x_scales, w_words, w_scal
                     project(blk, s, bank, 0, PASSES)
                 if blk == 0 and s == 0:
                     turn_bias_and_gain()
-                group_u.append(evacuate(bank, blk, s, acc, blk < final_blk and s >= nslots - TURN_LAG))
+                if s >= LANES and s % LANES == 0:
+                    sq = work.tile([P, LANES, BANK], F32, name="sq", tag="sq", bufs=3)
+                group_u.append(evacuate(bank, blk, s, sq[:, s % LANES, :]))
+                if s >= LANES and s % LANES == LANES - 1:
+                    owed.append((acc, sq))
                 if chores:
                     chores[0]()
                     chores.remove(chores[0])
@@ -402,6 +402,6 @@ def tile_causalwanselfattention_pa_kernel(tc, x_words, x_scales, w_words, w_scal
             if blk == final_blk:
                 steps = [(t, part) for part in range(len(LAST_PIECES)) for t in range(nt)]
             for t, part in steps:
-                state["due"] = max(norm_due + 2, state["due"] + 1)
+                state["due"] = max(norm_due + (2 if blk == final_blk else FIN), state["due"] + 1)
                 later(state["due"], lambda blk=blk, t=t, part=part, pend=pend, rstd=rstd: finish(blk, t, part, pend, rstd))
         run_due(now, True)

@@ -131,16 +131,9 @@ def tile_causalwanselfattention_pa_kernel(tc, x_words, x_scales, w_words, w_scal
         load_w_codes(0, HALF, PASSES)
         nc.scalar.dma_start(out=bg_rows[0:CT, :], in_=b.rearrange("(c p) -> c p", p=P))
         nc.scalar.dma_start(out=bg_rows[32 : 32 + CT, :], in_=g.rearrange("(c p) -> c p", p=P))
-        load_w_scales(1)
-        load_w_scales(2)
-        load_w_codes(1)
-        load_w_codes(2)
-        load_w_scales(3)
-        load_w_scales(4)
-        load_w_scales(5)
-        load_w_codes(3)
-        load_w_codes(4)
-        load_w_codes(5)
+        for q in range(1, CT // QUARTERS):
+            load_w_scales(q)
+            load_w_codes(q)
         stage_scales(1)
         stage_codes(1)
         for step in table_steps(0):

@@ -115,7 +115,7 @@ def tile_causalwanselfattention_pa_kernel(tc, x_words, x_scales, w_words, w_scal
         nc.gpsimd.memset(eps[:], EPS)
         bg_rows = keep.tile([P, P], BF16, name="bg_rows")
         nc.gpsimd.memset(bg_rows[:], 0.0)
-        ident = keep.tile([P, P], F32, name="ident")
+        ident = keep.tile([P, P], F32, name="ident", align_bytes=256)
         make_identity(nc, ident[:])
         warm = keep.tile([P, 1], F32, name="warm")
         nc.scalar.activation(out=warm[:], in_=eps[:], func=ACT.Abs_reciprocal_sqrt)
@@ -174,7 +174,7 @@ def tile_causalwanselfattention_pa_kernel(tc, x_words, x_scales, w_words, w_scal
 
         def evacuate(bank, blk, s, sq):
             n = BLOCKS[blk]
-            u = work.tile([P, BANK], F32, name="u", tag="u", bufs=8)
+            u = work.tile([P, BANK], F32, name="u", tag="u", bufs=8, align_bytes=256)
             last_of_all = blk == final_blk and s == CT * n // BANK - 1
             for what in ("sq", "u") if last_of_all else ("u", "sq"):
                 for j in range(BANK // n):
@@ -189,7 +189,7 @@ def tile_causalwanselfattention_pa_kernel(tc, x_words, x_scales, w_words, w_scal
         def sum_of_squares(blk, sources, ssum, rstd):
             n = BLOCKS[blk]
             nt = n // P
-            junk = work.tile([P, P], BF16, name="junk", tag="junk", bufs=1)
+            junk = bg_rows
             sums = []
             if len(sources) == 1:
                 bank = psum.tile([P, BANK], F32, name="mx", tag="mx")

@@ -27,7 +27,8 @@ LAST_GROUPS = {128: (3, 2, 1), 256: (4, 4, 2, 2), 512: (4, 4, 4, 4, 4, 4)}
 TURN_LAG = 2
 ACT_W = 1024
 PARTS = 2
-ALL_ACT_FROM = 4
+FINE_BEFORE = 2
+FINE_PARTS = 4
 FIN = 4
 LANES = 2
 LAST_PIECES = ((0, 1024), (1024, 2048), (2048, 2560), (2560, 3072))
@@ -309,11 +310,12 @@ def tile_causalwanselfattention_pa_kernel(tc, x_words, x_scales, w_words, w_scal
                     nc.scalar.activation(out=mine[:, a0:a1], in_=mine[:, a0:a1], func=ACT.Copy, scale=r)
                 nc.sync.dma_start(out=out_rows[row0 : row0 + P, a0:a1], in_=mine[:, a0:a1])
                 return
-            act_w = DIM // PARTS if blk >= ALL_ACT_FROM else ACT_W
+            parts = FINE_PARTS if blk < FINE_BEFORE else PARTS
+            act_w = ACT_W * PARTS // parts
             a0 = act_w * part
             nc.scalar.activation(out=mine[:, a0 : a0 + act_w], in_=mine[:, a0 : a0 + act_w], func=ACT.Copy, scale=r)
-            if part == PARTS - 1:
-                v0 = act_w * PARTS
+            if part == parts - 1:
+                v0 = act_w * parts
                 if v0 < DIM:
                     nc.vector.tensor_scalar_mul(out=mine[:, v0:DIM], in0=mine[:, v0:DIM], scalar1=r)
                 nc.sync.dma_start(out=out_rows[row0 : row0 + P, :], in_=mine)
@@ -391,7 +393,7 @@ def tile_causalwanselfattention_pa_kernel(tc, x_words, x_scales, w_words, w_scal
                     group_u = []
                 run_due(now, False)
             norm_due = now + 2 * lag
-            steps = [(t, part) for t in range(nt) for part in range(PARTS)]
+            steps = [(t, part) for t in range(nt) for part in range(FINE_PARTS if blk < FINE_BEFORE else PARTS)]
             if blk == final_blk:
                 steps = [(t, part) for part in range(len(LAST_PIECES)) for t in range(nt)]
             for t, part in steps:

from contextlib import ExitStack

import concourse.mybir as mybir
from concourse.masks import make_identity

ROWS, DIM, HEAD = 2048, 3072, 256
FLOPS = 2 * ROWS * DIM * DIM
EPS = 1e-6

F32 = mybir.dt.float32
BF16 = mybir.dt.bfloat16
U8 = mybir.dt.uint8
I32 = mybir.dt.int32
FP4X4 = mybir.dt.float4_e2m1fn_x4
ACT = mybir.ActivationFunctionType
ALU = mybir.AluOpType
AX = mybir.AxisListType

P = 128
PASSES = DIM // 512
HALF = 2
CT = DIM // P
BANK = 512
QUARTERS = BANK // P
BLOCKS = (512, 512, 512, 256, 256)
LAST_GROUPS = {128: (3, 2, 1), 256: (4, 4, 2, 2), 512: (4, 4, 4, 4, 4, 4)}
TURN_LAG = 2
ACT_W = 1024
PARTS = 2
FINE_BEFORE = 2
FINE_PARTS = 4
FIN = 4
LANES = 2
LAST_PIECES = ((0, 1024), (1024, 2048), (2048, 2560), (2560, 3072))
LAST_SCALED_FROM = 2560
LAST_ADDS_BEFORE = 16


def tile_causalwanselfattention_pa_kernel(tc, x_words, x_scales, w_words, w_scales, b, g, freqs, out):
    nc = tc.nc
    out_rows = out.rearrange("r h d -> r (h d)")
    final_blk = len(BLOCKS) - 1

    with ExitStack() as ctx:
        keep = ctx.enter_context(tc.tile_pool(name="keep", bufs=1))
        work = ctx.enter_context(tc.tile_pool(name="work", bufs=2))
        psum = ctx.enter_context(tc.psum_pool(name="psum", bufs=4))
        ctx.enter_context(tc.manual_schedule())

        def load_scales(plane, src, span, fresh=True):
            if fresh:
                nc.vector.memset(plane[:].bitcast(I32), 0)
            for quad in range(4):
                nc.sync.dma_start(
                    out=plane[32 * quad : 32 * quad + 4, :, :].bitcast(I32),
                    in_=src[:, 4 * quad : 4 * quad + 4, span].rearrange("k r n -> r k n").bitcast(I32),
                )

        def load_codes(codes, src, span, k0=0, k1=PASSES):
            nc.sync.dma_start(out=codes[:, k0:k1, :].bitcast(I32), in_=src[k0:k1, :, span].rearrange("k p n -> p k n").bitcast(I32))

        starts = [sum(BLOCKS[:i]) for i in range(len(BLOCKS))]
        staged = {}
        for blk in range(len(BLOCKS)):
            staged[blk] = {}

        def stage_scales(blk):
            n = BLOCKS[blk]
            xs = work.tile([P, PASSES, n], U8, name="xs", tag="xs", bufs=2, align_bytes=256)
            load_scales(xs, x_scales, slice(starts[blk], starts[blk] + n), blk < 2)
            staged[blk]["xs"] = xs

        def stage_codes(blk, k0=0, k1=PASSES):
            n = BLOCKS[blk]
            if k0 == 0:
                xc = work.tile([P, PASSES, 2 * n], U8, name="xc", tag="xc", bufs=2, align_bytes=256)
                staged[blk]["xc"] = xc
            load_codes(staged[blk]["xc"], x_words, slice(2 * starts[blk], 2 * (starts[blk] + n)), k0, k1)

        tables = {}

        def stage_freqs(sb):
            fr = work.tile([P, QUARTERS, HEAD], BF16, name="fr", tag="fr", bufs=3)
            nc.gpsimd.dma_start(out=fr[:], in_=freqs[BANK * sb : BANK * (sb + 1), :].rearrange("(t p) d -> p t d", p=P))
            tables[sb] = {"fr": fr}

        def table_steps(sb):
            pairs = QUARTERS * HEAD // 2
            fr = tables[sb]["fr"][:].rearrange("p t (j e) -> p (t j) e", e=2)
            tab = work.tile([P, 2, QUARTERS, HEAD], BF16, name="tab", tag="tab", bufs=2)
            ccv = tab[:, 0, :, :].rearrange("p t (j e) -> p (t j) e", e=2)
            snv = tab[:, 1, :, :].rearrange("p t (j e) -> p (t j) e", e=2)
            tables[sb]["tab"] = tab

            return [
                lambda: nc.scalar.activation(out=ccv, in_=fr[:, :, 0:1].to_broadcast([P, pairs, 2]), func=ACT.Copy),
                lambda: nc.scalar.activation(out=snv[:, :, 0:1], in_=fr[:, :, 1:2], func=ACT.Copy),
                lambda: nc.scalar.activation(out=snv[:, :, 1:2], in_=fr[:, :, 1:2], func=ACT.Copy, scale=-1.0),
            ]

        wc = []
        ws = []
        for q in range(CT // QUARTERS):
            wcq = keep.tile([P, PASSES, 2 * BANK], U8, name="wc%d" % q, align_bytes=256)
            wsq = keep.tile([P, PASSES, BANK], U8, name="ws%d" % q, align_bytes=256)
            wc.append(wcq)
            ws.append(wsq)

        def load_w_scales(q):
            load_scales(ws[q], w_scales, slice(BANK * q, BANK * (q + 1)))

        def load_w_codes(q, k0=0, k1=PASSES):
            load_codes(wc[q], w_words, slice(2 * BANK * q, 2 * BANK * (q + 1)), k0, k1)

        eps = keep.tile([P, 1], F32, name="eps")
        nc.gpsimd.memset(eps[:], EPS)
        bg_rows = keep.tile([P, P], BF16, name="bg_rows")
        nc.gpsimd.memset(bg_rows[:], 0.0)
        ident = keep.tile([P, P], F32, name="ident", align_bytes=256)
        make_identity(nc, ident[:])
        warm = keep.tile([P, 1], F32, name="warm")
        nc.scalar.activation(out=warm[:], in_=eps[:], func=ACT.Abs_reciprocal_sqrt)

        stage_freqs(0)
        stage_freqs(1)
        stage_freqs(2)
        stage_codes(0, 0, HALF)
        load_w_codes(0, 0, HALF)
        load_w_scales(0)
        stage_scales(0)
        stage_codes(0, HALF, PASSES)
        load_w_codes(0, HALF, PASSES)
        nc.scalar.dma_start(out=bg_rows[0:CT, :], in_=b.rearrange("(c p) -> c p", p=P))
        nc.scalar.dma_start(out=bg_rows[32 : 32 + CT, :], in_=g.rearrange("(c p) -> c p", p=P))
        for q in range(1, CT // QUARTERS):
            load_w_scales(q)
            load_w_codes(q)
        stage_scales(1)
        stage_codes(1)
        for step in table_steps(0):
            step()

        bg_f32 = keep.tile([P, P], F32, name="bg_f32")
        nc.vector.tensor_copy(out=bg_f32[:], in_=bg_rows[:])
        cols = keep.tile([P, P], F32, name="cols")
        bgcol = keep.tile([P, CT], F32, name="bgcol")
        flag = keep.tile([P, 1], F32, name="flag")

        def turn_bias_and_gain():
            bank = psum.tile([P, BANK], F32, name="tr", tag="tr")
            nc.tensor.transpose(out=bank[:, 0:P], in_=bg_f32[:], identity=ident[:])
            nc.vector.tensor_copy(out=cols[:], in_=bank[:, 0:P])
            nc.vector.tensor_tensor(out=bgcol[:], in0=cols[:, 0:CT], in1=cols[:, 32 : 32 + CT], op=ALU.mult)

        owed = []
        complete = []
        chores = []

        def project(blk, s, bank, k0, k1):
            n = BLOCKS[blk]
            xc = staged[blk]["xc"]
            xs = staged[blk]["xs"]
            for j in range(BANK // n):
                q, i = divmod(s * (BANK // n) + j, QUARTERS)
                for k in range(k0, k1):
                    nc.tensor.matmul_mx(
                        out=bank[:, n * j : n * (j + 1)],
                        lhsT=wc[q][:, k, 2 * P * i : 2 * P * (i + 1)].bitcast(FP4X4),
                        lhsT_scale=ws[q][:, k, P * i : P * (i + 1)],
                        rhs=xc[:, k, :].bitcast(FP4X4),
                        rhs_scale=xs[:, k, :],
                        start=(k == 0),
                        stop=(k == PASSES - 1),
                    )

        def evacuate(bank, blk, s, sq):
            n = BLOCKS[blk]
            u = work.tile([P, BANK], F32, name="u", tag="u", bufs=8, align_bytes=256)
            last_of_all = blk == final_blk and s == CT * n // BANK - 1
            for what in ("sq", "u") if last_of_all else ("u", "sq"):
                for j in range(BANK // n):
                    c = s * (BANK // n) + j
                    span = slice(n * j, n * (j + 1))
                    if what == "u":
                        nc.scalar.activation(out=u[:, span], in_=bank[:, span], func=ACT.Identity, bias=bgcol[:, c : c + 1], scale=cols[:, 32 + c : 33 + c])
                    else:
                        nc.scalar.activation(out=sq[:, span], in_=bank[:, span], func=ACT.Square, bias=cols[:, c : c + 1], scale=1.0)
            return u

        def sum_of_squares(blk, sources, ssum, rstd):
            n = BLOCKS[blk]
            nt = n // P
            junk = bg_rows
            sums = []
            if len(sources) == 1:
                bank = psum.tile([P, BANK], F32, name="mx", tag="mx")
                for t in range(nt):
                    sums.append(bank[:, P * t : P * (t + 1)])
            else:
                for t in range(nt):
                    bank = psum.tile([P, BANK], F32, name="mx", tag="mx")
                    sums.append(bank[:, 0:P])
            per_slot = BANK // n
            if len(sources) == 1:
                order = [(0, t, j) for t in range(nt) for j in range(per_slot)]
            else:
                order = [(i, t, j) for i in range(len(sources)) for t in range(nt) for j in range(per_slot)]
            for i, t, j in order:
                nc.tensor.matmul(
                    out=sums[t], lhsT=sources[i][:, n * j + P * t : n * j + P * (t + 1)], rhs=ident[:], is_transpose=True,
                    start=(i == 0 and j == 0), stop=(i == len(sources) - 1 and j == per_slot - 1),
                )
            for t in range(nt):
                nc.scalar.activation(out=junk[:], in_=sums[t], func=ACT.Copy, accum_out=ssum[:, t : t + 1])
            nc.scalar.activation(out=rstd[:, 0:nt], in_=ssum[:, 0:nt], func=ACT.Abs_reciprocal_sqrt, bias=eps[:], scale=1.0 / DIM)

        def turn_to_tokens(blk, c0, group_u, closing, acc, ssum, rstd, carry):
            n = BLOCKS[blk]
            nt = n // P
            per_slot = BANK // n
            tab = tables[starts[blk] // BANK]["tab"][:, :, starts[blk] % BANK // P : (starts[blk] % BANK + n) // P, :]
            tail = closing and blk == final_blk
            if tail:
                sum_of_squares(blk, [x[:, i, :] for x in [acc] + [sq for a, sq in owed] for i in range(LANES)], ssum, rstd)
                owed.clear()
            banks = []
            for m in range(len(group_u) * per_slot // QUARTERS):
                for t in range(nt):
                    bank = psum.tile([P, BANK], F32, name="tr", tag="tr")
                    for i in range(QUARTERS):
                        si, j = divmod(QUARTERS * m + i, per_slot)
                        nc.tensor.transpose(out=bank[:, P * i : P * (i + 1)], in_=group_u[si][:, n * j + P * t : n * j + P * (t + 1)], identity=ident[:])
                    banks.append((bank, t))

            for b2, a2, ss2, rs2 in complete:
                sum_of_squares(b2, [a2[:, 0, :]], ss2, rs2)
            complete.clear()
            room = len(banks) // LANES if blk < final_blk or c0 < LAST_ADDS_BEFORE else 0
            mine = owed[:room]
            for job in mine:
                owed.remove(job)
            if mine:
                nc.vector.tensor_copy(out=flag[:], in_=mine[0][0][:, 0, 0:1])
            for a, sq in mine:
                nc.gpsimd.tensor_tensor(out=a[:], in0=a[:], in1=sq[:], op=ALU.add)
            if closing and not tail:
                nc.gpsimd.tensor_tensor(out=acc[:, 0, :], in0=acc[:, 0, :], in1=acc[:, 1, :], op=ALU.add)
                complete.append((blk, acc, ssum, rstd))
            prods = work.tile([P, QUARTERS, 2, BANK], F32, name="prods", tag="prods", bufs=1)
            for i in range(len(banks)):
                bank, t = banks[i]
                if tail:
                    for a in range(2):
                        nc.vector.scalar_tensor_tensor(
                            out=prods[:, i, a, :].rearrange("p (h d) -> p h d", d=HEAD),
                            in0=bank[:].rearrange("p (h d) -> p h d", d=HEAD),
                            scalar=rstd[:, t : t + 1],
                            in1=tab[:, a, t, :].unsqueeze(1).to_broadcast([P, BANK // HEAD, HEAD]),
                            op0=ALU.mult,
                            op1=ALU.mult,
                        )
                else:
                    nc.vector.tensor_tensor(
                        out=prods[:, i, :, :].rearrange("p a (h d) -> p a h d", d=HEAD),
                        in0=bank[:].unsqueeze(1).to_broadcast([P, 2, BANK]).rearrange("p a (h d) -> p a h d", d=HEAD),
                        in1=tab[:, :, t, :].unsqueeze(2).to_broadcast([P, 2, BANK // HEAD, HEAD]),
                        op=ALU.mult,
                    )
            carry["prods"] = prods
            carry["banks"] = len(banks)

        def rotate(blk, c0, pend, carry):
            nt = BLOCKS[blk] // P
            t0 = starts[blk] % BANK // P
            prods = carry["prods"]
            chunk0 = c0 // QUARTERS
            if nt == 1:
                k = carry["banks"]
                nc.vector.tensor_tensor(
                    out=pend[:, t0, BANK * chunk0 : BANK * (chunk0 + k)].rearrange("p (m n e) -> p m n e", m=k, e=2),
                    in0=prods[:, 0:k, 0, :].rearrange("p m (n e) -> p m n e", e=2),
                    in1=prods[:, 0:k, 1, :].rearrange("p m (n e) -> p m n e", e=2)[:, :, :, ::-1],
                    op=ALU.add,
                )
            elif nt == 2:
                k = carry["banks"] // nt
                for t in range(nt):
                    nc.vector.tensor_tensor(
                        out=pend[:, t0 + t, BANK * chunk0 : BANK * (chunk0 + k)].rearrange("p (m n e) -> p m n e", m=k, e=2),
                        in0=prods[:, t : nt * k : nt, 0, :].rearrange("p m (n e) -> p m n e", e=2),
                        in1=prods[:, t : nt * k : nt, 1, :].rearrange("p m (n e) -> p m n e", e=2)[:, :, :, ::-1],
                        op=ALU.add,
                    )
            else:
                for m in range(carry["banks"] // nt):
                    nc.vector.tensor_tensor(
                        out=pend[:, t0 : t0 + nt, BANK * (chunk0 + m) : BANK * (chunk0 + m + 1)].rearrange("p t (n e) -> p t n e", e=2),
                        in0=prods[:, nt * m : nt * (m + 1), 0, :].rearrange("p t (n e) -> p t n e", e=2),
                        in1=prods[:, nt * m : nt * (m + 1), 1, :].rearrange("p t (n e) -> p t n e", e=2)[:, :, :, ::-1],
                        op=ALU.add,
                    )

        def finish(blk, t, part, pend, rstd):
            r = rstd[:, t : t + 1]
            row0 = starts[blk] + P * t
            mine = pend[:, starts[blk] % BANK // P + t, :]
            if blk == final_blk:
                a0, a1 = LAST_PIECES[part]
                if a1 <= LAST_SCALED_FROM:
                    nc.scalar.activation(out=mine[:, a0:a1], in_=mine[:, a0:a1], func=ACT.Copy, scale=r)
                nc.sync.dma_start(out=out_rows[row0 : row0 + P, a0:a1], in_=mine[:, a0:a1])
                return
            parts = FINE_PARTS if blk < FINE_BEFORE else PARTS
            act_w = ACT_W * PARTS // parts
            a0 = act_w * part
            nc.scalar.activation(out=mine[:, a0 : a0 + act_w], in_=mine[:, a0 : a0 + act_w], func=ACT.Copy, scale=r)
            if part == parts - 1:
                v0 = act_w * parts
                if v0 < DIM:
                    nc.vector.tensor_scalar_mul(out=mine[:, v0:DIM], in0=mine[:, v0:DIM], scalar1=r)
                nc.sync.dma_start(out=out_rows[row0 : row0 + P, :], in_=mine)

        todo = []
        state = {"serial": 0, "due": 0}

        def later(due, fn):
            todo.append([due, state["serial"], fn])
            state["serial"] += 1

        def run_due(now, everything):
            ready = [e for e in todo if everything or e[0] <= now]
            for e in sorted(ready, key=lambda e: (e[0], e[1])):
                e[2]()
                todo.remove(e)

        now = 0
        first_banks = []
        for blk, n in enumerate(BLOCKS):
            nt = n // P
            nslots = CT * n // BANK
            if blk == final_blk:
                sizes = LAST_GROUPS[n]
            else:
                sizes = (4,) * (nslots // 4) if nslots % 4 == 0 else (3,) * (nslots // 3)
            lag = 1 if blk == final_blk else TURN_LAG
            if starts[blk] % BANK == 0:
                pend = work.tile([P, QUARTERS, DIM], F32, name="pend", tag="pend", bufs=2)
            acc = work.tile([P, LANES, BANK], F32, name="acc", tag="acc", bufs=2)
            sq = acc
            ssum = work.tile([P, QUARTERS], F32, name="ssum", tag="ssum", bufs=3)
            rstd = work.tile([P, QUARTERS], F32, name="rstd", tag="rstd", bufs=4)
            group_u = []
            done_groups = 0
            c0 = 0
            for s in range(nslots):
                if s == 0 and 1 <= blk < final_blk:
                    stage_scales(blk + 1)
                    stage_codes(blk + 1)
                sb = starts[blk] // BANK
                if s == 0 and starts[blk] % BANK == 0 and 1 <= sb < ROWS // BANK - 2:
                    stage_freqs(sb + 2)
                if s == 4 and starts[blk] % BANK == 0 and sb < ROWS // BANK - 1:
                    chores.extend(table_steps(sb + 1))
                if blk == 0 and s == 0:
                    for s2 in range(QUARTERS):
                        early = psum.tile([P, BANK], F32, name="mx", tag="mx")
                        first_banks.append(early)
                        project(0, s2, early, 0, HALF)
                if blk == 0 and s < QUARTERS:
                    bank = first_banks[s]
                    project(0, s, bank, HALF, PASSES)
                else:
                    bank = psum.tile([P, BANK], F32, name="mx", tag="mx")
                    project(blk, s, bank, 0, PASSES)
                if blk == 0 and s == 0:
                    turn_bias_and_gain()
                if s >= LANES and s % LANES == 0:
                    sq = work.tile([P, LANES, BANK], F32, name="sq", tag="sq", bufs=3)
                group_u.append(evacuate(bank, blk, s, sq[:, s % LANES, :]))
                if s >= LANES and s % LANES == LANES - 1:
                    owed.append((acc, sq))
                if chores:
                    chores[0]()
                    chores.remove(chores[0])
                now += 1
                if len(group_u) == sizes[done_groups]:
                    done_groups += 1
                    closing = done_groups == len(sizes)
                    carry = {}
                    later(now + lag, lambda blk=blk, c0=c0, gu=group_u, closing=closing, acc=acc, ssum=ssum, rstd=rstd, carry=carry: turn_to_tokens(blk, c0, gu, closing, acc, ssum, rstd, carry))
                    later(now + 2 * lag, lambda blk=blk, c0=c0, pend=pend, carry=carry: rotate(blk, c0, pend, carry))
                    c0 += len(group_u) * BANK // n
                    group_u = []
                run_due(now, False)
            norm_due = now + 2 * lag
            steps = [(t, part) for t in range(nt) for part in range(FINE_PARTS if blk < FINE_BEFORE else PARTS)]
            if blk == final_blk:
                steps = [(t, part) for part in range(len(LAST_PIECES)) for t in range(nt)]
            for t, part in steps:
                state["due"] = max(norm_due + (2 if blk == final_blk else FIN), state["due"] + 1)
                later(state["due"], lambda blk=blk, t=t, part=part, pend=pend, rstd=rstd: finish(blk, t, part, pend, rstd))
        run_due(now, True)
